import numpy as np
import ml_dtypes


def mxq(x, axis, fmt="e4m3"):
    dtype, down = {"e4m3": (ml_dtypes.float8_e4m3fn, 7), "e5m2": (ml_dtypes.float8_e5m2, 14)}[fmt]
    v = np.moveaxis(np.asarray(x, np.float32).astype(ml_dtypes.bfloat16).astype(np.float64), axis, -1)
    blocks = v.reshape(v.shape[:-1] + (-1, 32))
    amax = np.abs(blocks).max(-1, keepdims=True)
    byte = np.maximum(np.where(amax > 0, np.frexp(amax)[1] - 1 + 127, 0) - down, 1)
    scale = np.exp2(byte - 127.0)
    codes = (blocks / scale).astype(np.float32).astype(dtype).astype(np.float64)
    return np.moveaxis((codes * scale).reshape(v.shape), -1, axis)


WIDE = False


def mx_kscale(k):
    if not WIDE:
        return np.ones(k)
    levels = np.array([10, -10, 5, -5, 0])
    a = np.random.permutation(np.resize(levels, k // 512 * 4)).reshape(k // 512, 4)
    idx = np.arange(k)
    return np.exp2(a[idx // 512, idx % 128 // 32])


BF16 = ml_dtypes.bfloat16


def bf(x):
    return np.asarray(x, np.float32).astype(BF16)


def f64(x):
    return np.asarray(x).astype(np.float64)


E2M1 = np.array([0.0, 0.5, 1.0, 1.5, 2.0, 3.0, 4.0, 6.0, -0.0, -0.5, -1.0, -1.5, -2.0, -3.0, -4.0, -6.0])


def pack_weight(w, fmt):
    k, n = w.shape
    w = f64(bf(w)).reshape(k // 32, 32, n)
    amax = np.abs(w).max(1)
    if fmt == "e4m3":
        byte = np.frexp(amax)[1] - 1 + 127 - 7
    else:
        mant, ex = np.frexp(amax / 6.0)
        byte = np.where(mant > 0.5, ex, ex - 1) + 127
    byte = np.clip(np.where(amax > 0, byte, 1), 1, 254)
    scaled = (w * np.exp2(127.0 - byte)[:, None, :]).reshape(k, n).astype(np.float32)
    by_word = np.ascontiguousarray(scaled.reshape(k // 512, 128, 4, n).transpose(0, 1, 3, 2))
    if fmt == "e4m3":
        words = by_word.astype(ml_dtypes.float8_e4m3fn).view(np.uint8)
    else:
        c = by_word.astype(ml_dtypes.float4_e2m1fn).view(np.uint8) & 0xF
        words = c[..., 0::2] | (c[..., 1::2] << 4)
    return np.ascontiguousarray(words), np.ascontiguousarray(byte.astype(np.uint8).reshape(k // 512, 16, n))


def unpack_weight(words, scales, fmt):
    g, p, n, _ = words.shape
    if fmt == "e4m3":
        vals = np.ascontiguousarray(words).view(ml_dtypes.float8_e4m3fn).astype(np.float64)
    else:
        nib = np.empty((g, p, n, 4), np.uint8)
        nib[..., 0::2] = words & 0xF
        nib[..., 1::2] = words >> 4
        vals = E2M1[nib]
    vals = vals * np.repeat(np.exp2(scales.astype(np.float64) - 127.0), 8, axis=1)[..., None]
    return vals.transpose(0, 1, 3, 2).reshape(g * 512, n)

def pack4(w):
    words, scales = pack_weight(w, "e2m1")
    return words.reshape(words.shape[0], 128, -1), scales


def unpack4(words, scales):
    return unpack_weight(words.reshape(words.shape[0], 128, -1, 2), scales, "e2m1")


N, G, GIN, GOUT = 1024, 8, 512, 512

P0 = np.array([0.5, 1.0, 0.5, 0.3])
Q0 = np.array([0.5, 0.3, 0.2])


def rational(y, p, q):
    p = p[None, :, :, None]
    q = q[None, :, :, None]
    y2 = y * y
    y3 = y2 * y
    num = p[:, :, 0] + p[:, :, 1] * y + p[:, :, 2] * y2 + p[:, :, 3] * y3
    den = 1.0 + np.abs(q[:, :, 0] * y + q[:, :, 1] * y2 + q[:, :, 2] * y3)
    return num / den


def setup_inputs():
    s = mx_kscale(GIN)
    x = bf(np.random.standard_normal((N, G * GIN)) * np.tile(s, G))
    stack = np.random.standard_normal((G, GIN, GOUT)) / np.sqrt(GIN) / s[None, :, None]
    W_words, W_scales = pack4(stack.reshape(-1, GOUT))
    return {"x": x,
            "W_words": W_words,
            "W_scales": W_scales,
            "b": bf(np.random.standard_normal((G, GOUT)) * 0.3),
            "p": bf(P0 + 0.1 * np.random.standard_normal((G, P0.size))),
            "q": bf(Q0 + 0.05 * np.random.standard_normal((G, Q0.size)))}


def reference(x, W_words, W_scales, b, p, q):
    n = x.shape[0]
    xg = f64(x).reshape(n, G, GIN)
    xq = mxq(xg, 2, "e4m3")
    wq = unpack4(W_words, W_scales).reshape(G, GIN, GOUT)
    y = (xq.transpose(1, 0, 2) @ wq).transpose(1, 0, 2) + f64(b)[None]
    out = rational(y, f64(p), f64(q))
    return out.reshape(n, G * GOUT)

@@ -1,0 +1,240 @@
+from contextlib import ExitStack
+
+import concourse.mybir as mybir
+from concourse.masks import make_identity
+
+F32 = mybir.dt.float32
+BF16 = mybir.dt.bfloat16
+I32 = mybir.dt.int32
+U8 = mybir.dt.uint8
+U32 = mybir.dt.uint32
+FP8X4 = mybir.dt.float8_e4m3fn_x4
+FP4X4 = mybir.dt.float4_e2m1fn_x4
+ACT = mybir.ActivationFunctionType
+ALU = mybir.AluOpType
+
+P = 128
+ROWS = 1024
+GROUPS = 8
+GIN = 512
+GOUT = 512
+HALF = 512
+ROW_TILES = HALF // P
+OUT_TILES = GOUT // P
+BLOCKS = GROUPS * (ROWS // HALF)
+TILES = BLOCKS * OUT_TILES
+
+FLOPS = 2 * ROWS * GROUPS * GIN * GOUT
+
+
+def tile_groupkanlayer_e_kernel(tc, x, W_words, W_scales, b, p, q, out):
+    nc = tc.nc
+    with ExitStack() as ctx:
+        const = ctx.enter_context(tc.tile_pool(name="const", bufs=1))
+        work = ctx.enter_context(tc.tile_pool(name="work", bufs=2))
+        psum = ctx.enter_context(tc.psum_pool(name="psum", bufs=2))
+        ctx.enter_context(tc.manual_schedule())
+
+        x_blks, x_turned, x_grouped, x_codes, x_scales = {}, {}, {}, {}, {}
+        s_ps, y_sb, n1_sb, d1_sb, n2_sb, d2_sb, n3_sb, d3_sb = {}, {}, {}, {}, {}, {}, {}, {}
+        num_ps, den_ps, a_sb, u_sb, r_sb, stage = {}, {}, {}, {}, {}, {}
+
+        def load_x(blk):
+            g, half = divmod(blk, ROWS // HALF)
+            x_blks[blk] = work.tile([P, ROW_TILES, GIN], BF16, name="x_blk", bufs=4)
+            rows = x[half * HALF : (half + 1) * HALF, g * GIN : (g + 1) * GIN]
+            nc.sync.dma_start(out=x_blks[blk][:], in_=rows.rearrange("(a r) k -> r a k", r=P))
+
+        def turn_x(blk, h):
+            words = x_blks[blk][:].bitcast(F32)
+            x_turned[(blk, h)] = psum.tile([P, 2, 2, P], F32, name="x_turned")
+            for a in range(2):
+                for u in range(2):
+                    nc.tensor.transpose(
+                        x_turned[(blk, h)][:, a, u, :], words[:, 2 * h + a, u : GIN // 2 : 2], ident[:]
+                    )
+
+        def group_x(blk, h):
+            if h == 0:
+                x_grouped[blk] = work.tile([P, 4 * HALF], BF16, name="x_grouped", align_bytes=64)
+            dst = x_grouped[blk][:].bitcast(F32).rearrange("p (a n u) -> p a n u", a=ROW_TILES, u=2)
+            nc.scalar.copy(
+                out=dst[:, 2 * h : 2 * h + 2],
+                in_=x_turned[(blk, h)][:].rearrange("p a u n -> p a n u"),
+            )
+
+        def quantise_x(blk):
+            x_codes[blk] = work.tile([P, HALF], U32, name="x_codes", align_bytes=64)
+            x_scales[blk] = work.tile([P, HALF], U8, name="x_scales", align_bytes=64)
+            nc.vector.quantize_mx(
+                out=x_codes[blk][:].bitcast(FP8X4), scales=x_scales[blk][:], in_=x_grouped[blk][:]
+            )
+
+        def where(t):
+            blk, ot = divmod(t, OUT_TILES)
+            return blk, ot, blk // (ROWS // HALF)
+
+        def coef(table, width, g, i):
+            return table[:, width * g + i : width * g + i + 1]
+
+        def chain_tile(store, t, name, bufs):
+            store[t] = work.tile([P, HALF], F32, name=name, bufs=bufs)
+            return store[t]
+
+        def multiply(t):
+            blk, ot, g = where(t)
+            s_ps[t] = psum.tile([P, HALF], F32, name="s_ps")
+            nc.tensor.matmul_mx(
+                out=s_ps[t][:],
+                lhsT=w_words[:, g, 2 * P * ot : 2 * P * (ot + 1)].bitcast(FP4X4),
+                lhsT_scale=w_planes[:, g, P * ot : P * (ot + 1)],
+                rhs=x_codes[blk][:].bitcast(FP8X4),
+                rhs_scale=x_scales[blk][:],
+                start=True,
+                stop=True,
+            )
+
+        def add_bias(t):
+            blk, ot, g = where(t)
+            nc.scalar.activation(
+                out=chain_tile(y_sb, t, "y", 3)[:], in_=s_ps[t][:], func=ACT.Identity,
+                bias=coef(b_cols, OUT_TILES, g, ot), scale=1.0,
+            )
+
+        def den_linear(t):
+            g = where(t)[2]
+            nc.scalar.activation(
+                out=chain_tile(d1_sb, t, "d1", 3)[:], in_=y_sb[t][:], func=ACT.Identity,
+                bias=coef(q_f32, 3, g, 1), scale=coef(q_f32, 3, g, 2),
+            )
+
+        def num_linear(t):
+            g = where(t)[2]
+            nc.vector.tensor_scalar(
+                out=chain_tile(n1_sb, t, "n1", 2)[:], in0=y_sb[t][:],
+                scalar1=coef(p_f32, 4, g, 3), scalar2=coef(p_f32, 4, g, 2), op0=ALU.mult, op1=ALU.add,
+            )
+
+        def times_y(dst, src, t, name):
+            nc.vector.tensor_tensor(
+                out=chain_tile(dst, t, name, 2)[:], in0=src[t][:], in1=y_sb[t][:], op=ALU.mult
+            )
+
+        def plus_times_y(dst, src, t, name, bufs, c):
+            nc.vector.scalar_tensor_tensor(
+                out=chain_tile(dst, t, name, bufs)[:], in0=src[t][:], scalar=c, in1=y_sb[t][:],
+                op0=ALU.add, op1=ALU.mult,
+            )
+
+        def turn_back(dst, src, t, name):
+            dst[t] = psum.tile([P, ROW_TILES, P], F32, name=name)
+            for a in range(ROW_TILES):
+                nc.tensor.transpose(dst[t][:, a, :], src[t][:, a * P : (a + 1) * P], ident[:])
+
+        def finish(t):
+            blk, ot, g = where(t)
+            if ot == 0:
+                stage[blk] = work.tile([P, ROW_TILES, GOUT], F32, name="stage", bufs=3)
+            nc.vector.scalar_tensor_tensor(
+                out=stage[blk][:, :, ot * P : (ot + 1) * P], in0=num_ps[t][:], scalar=coef(p_f32, 4, g, 0),
+                in1=r_sb[t][:].rearrange("p (a o) -> p a o", a=ROW_TILES), op0=ALU.add, op1=ALU.mult,
+            )
+            if ot == OUT_TILES - 1:
+                half = blk % (ROWS // HALF)
+                rows = out[half * HALF : (half + 1) * HALF, g * GOUT : (g + 1) * GOUT]
+                nc.sync.dma_start(out=rows.rearrange("(a r) o -> r a o", r=P), in_=stage[blk][:])
+
+        load_x(0)
+
+        w_planes = const.tile([P, GROUPS, GOUT], U8, align_bytes=64)
+        nc.vector.memset(w_planes[:].bitcast(I32), 0)
+        b_rows = const.tile([P, P], BF16)
+        nc.vector.memset(b_rows[:], 0.0)
+        one = const.tile([P, 1], F32)
+        nc.vector.memset(one[:], 1.0)
+        for quad in range(4):
+            nc.sync.dma_start(
+                out=w_planes[32 * quad : 32 * quad + 4].bitcast(I32),
+                in_=W_scales.bitcast(I32)[:, 4 * quad : 4 * quad + 4, :].rearrange("g r n -> r g n"),
+            )
+        w_words = const.tile([P, GROUPS, 2 * GOUT], U8, align_bytes=64)
+        w_dram = W_words.bitcast(I32).rearrange("g pp w -> pp g w")
+        nc.sync.dma_start(out=w_words[:, 0:1, :].bitcast(I32), in_=w_dram[:, 0:1, :])
+        load_x(1)
+        nc.sync.dma_start(out=w_words[:, 1:GROUPS, :].bitcast(I32), in_=w_dram[:, 1:GROUPS, :])
+
+        ident = const.tile([P, P], F32)
+        make_identity(nc, ident[:])
+
+        p_bf = const.tile([P, GROUPS * 4], BF16)
+        q_bf = const.tile([P, GROUPS * 3], BF16)
+        nc.scalar.dma_start(out=p_bf[:], in_=p.rearrange("g c -> (g c)").partition_broadcast(P))
+        nc.scalar.dma_start(out=q_bf[:], in_=q.rearrange("g c -> (g c)").partition_broadcast(P))
+        p_f32 = const.tile([P, GROUPS * 4], F32)
+        q_f32 = const.tile([P, GROUPS * 3], F32)
+        nc.vector.tensor_copy(out=p_f32[:], in_=p_bf[:])
+        nc.vector.tensor_copy(out=q_f32[:], in_=q_bf[:])
+
+        nc.scalar.dma_start(
+            out=b_rows[0 : GROUPS * OUT_TILES, :], in_=b.rearrange("g (ot o) -> (g ot) o", o=P)
+        )
+        b_rows_f32 = const.tile([P, P], F32)
+        nc.vector.tensor_copy(out=b_rows_f32[:], in_=b_rows[:])
+        b_turned = psum.tile([P, HALF], F32, name="s_ps")
+        nc.tensor.transpose(b_turned[:, 0:P], b_rows_f32[:], ident[:])
+        b_cols = const.tile([P, GROUPS * OUT_TILES], F32)
+        nc.vector.tensor_copy(out=b_cols[:], in_=b_turned[:, 0 : GROUPS * OUT_TILES])
+
+        def live(t):
+            return 0 <= t < TILES
+
+        for step in range(-OUT_TILES, TILES + 4):
+            next_blk, phase = step // OUT_TILES + 1, step % OUT_TILES
+            prepare = next_blk < BLOCKS
+            t_in, t_poly, t_den, t_num, t_out = step, step - 1, step - 2, step - 3, step - 4
+
+            if phase == 0 and next_blk + 2 < BLOCKS:
+                load_x(next_blk + 2)
+
+            if phase == 3 and prepare:
+                quantise_x(next_blk)
+            if live(t_poly):
+                g = where(t_poly)[2]
+                num_linear(t_poly)
+                times_y(d2_sb, d1_sb, t_poly, "d2")
+            if live(t_out):
+                finish(t_out)
+            if live(t_poly):
+                times_y(n2_sb, n1_sb, t_poly, "n2")
+                plus_times_y(d3_sb, d2_sb, t_poly, "d3", 3, coef(q_f32, 3, g, 0))
+                plus_times_y(n3_sb, n2_sb, t_poly, "n3", 4, coef(p_f32, 4, g, 1))
+
+            if live(t_num):
+                nc.scalar.activation(
+                    out=chain_tile(a_sb, t_num, "a", 2)[:],
+                    in_=den_ps[t_num][:].rearrange("p a o -> p (a o)"), func=ACT.Abs,
+                )
+            if live(t_in):
+                add_bias(t_in)
+            if live(t_num):
+                nc.scalar.activation(
+                    out=chain_tile(u_sb, t_num, "u", 2)[:], in_=a_sb[t_num][:],
+                    func=ACT.Abs_reciprocal_sqrt, bias=one[:, 0:1], scale=1.0,
+                )
+            if live(t_in):
+                den_linear(t_in)
+            if live(t_num):
+                nc.scalar.activation(
+                    out=chain_tile(r_sb, t_num, "r", 3)[:], in_=u_sb[t_num][:], func=ACT.Square
+                )
+            if phase in (1, 2) and prepare:
+                group_x(next_blk, phase - 1)
+
+            if live(t_den):
+                turn_back(den_ps, d3_sb, t_den, "den_ps")
+            if live(t_num):
+                turn_back(num_ps, n3_sb, t_num, "num_ps")
+            if phase in (0, 1) and prepare:
+                turn_x(next_blk, phase)
+            if live(t_in + 1):
+                multiply(t_in + 1)

@@ -19,10 +19,15 @@ GROUPS = 8
 GIN = 512
 GOUT = 512
 HALF = 512
+HALVES = ROWS // HALF
 ROW_TILES = HALF // P
 OUT_TILES = GOUT // P
-BLOCKS = GROUPS * (ROWS // HALF)
+BLOCKS = GROUPS * HALVES
 TILES = BLOCKS * OUT_TILES
+PIECES = BLOCKS * ROW_TILES
+
+AT_LOAD, AT_TURN_X, AT_GROUP_X, AT_QUANTISE = -15, -7, -6, -5
+AT_MULTIPLY, AT_BIAS, AT_POLY, AT_TURN_DEN, AT_RECIPROCAL, AT_TURN_NUM, AT_FINISH = -1, 0, 2, 4, 5, 6, 7
 
 FLOPS = 2 * ROWS * GROUPS * GIN * GOUT
 
@@ -35,44 +40,43 @@ def tile_groupkanlayer_e_kernel(tc, x, W_words, W_scales, b, p, q, out):
         psum = ctx.enter_context(tc.psum_pool(name="psum", bufs=2))
         ctx.enter_context(tc.manual_schedule())
 
-        x_blks, x_turned, x_grouped, x_codes, x_scales = {}, {}, {}, {}, {}
+        x_rows, x_turned, x_grouped, x_codes, x_scales = {}, {}, {}, {}, {}
         s_ps, y_sb, n1_sb, d1_sb, n2_sb, d2_sb, n3_sb, d3_sb = {}, {}, {}, {}, {}, {}, {}, {}
-        num_ps, den_ps, a_sb, u_sb, r_sb, stage = {}, {}, {}, {}, {}, {}
+        num_ps, den_ps, a_sb, u_sb, r_sb = {}, {}, {}, {}, {}
 
-        def load_x(blk):
-            g, half = divmod(blk, ROWS // HALF)
-            x_blks[blk] = work.tile([P, ROW_TILES, GIN], BF16, name="x_blk", bufs=4)
-            rows = x[half * HALF : (half + 1) * HALF, g * GIN : (g + 1) * GIN]
-            nc.sync.dma_start(out=x_blks[blk][:], in_=rows.rearrange("(a r) k -> r a k", r=P))
+        def load_x(j):
+            blk, a = divmod(j, ROW_TILES)
+            g, half = divmod(blk, HALVES)
+            row0 = half * HALF + a * P
+            x_rows[j] = work.tile([P, GIN], BF16, name="x_rows", bufs=AT_TURN_X - AT_LOAD + 2)
+            nc.sync.dma_start(out=x_rows[j][:], in_=x[row0 : row0 + P, g * GIN : (g + 1) * GIN])
 
-        def turn_x(blk, h):
-            words = x_blks[blk][:].bitcast(F32)
-            x_turned[(blk, h)] = psum.tile([P, 2, 2, P], F32, name="x_turned")
-            for a in range(2):
-                for u in range(2):
-                    nc.tensor.transpose(
-                        x_turned[(blk, h)][:, a, u, :], words[:, 2 * h + a, u : GIN // 2 : 2], ident[:]
-                    )
+        def turn_x(j):
+            words = x_rows[j][:].bitcast(F32)
+            x_turned[j] = psum.tile([P, 2, P], F32, name="x_turned")
+            for u in range(2):
+                nc.tensor.transpose(x_turned[j][:, u, :], words[:, u : GIN // 2 : 2], ident[:])
 
-        def group_x(blk, h):
-            if h == 0:
-                x_grouped[blk] = work.tile([P, 4 * HALF], BF16, name="x_grouped", align_bytes=64)
-            dst = x_grouped[blk][:].bitcast(F32).rearrange("p (a n u) -> p a n u", a=ROW_TILES, u=2)
+        def group_x(j):
+            x_grouped[j] = work.tile([P, 4 * P], BF16, name="x_grouped", bufs=3, align_bytes=64)
             nc.scalar.copy(
-                out=dst[:, 2 * h : 2 * h + 2],
-                in_=x_turned[(blk, h)][:].rearrange("p a u n -> p a n u"),
+                out=x_grouped[j][:].bitcast(F32).rearrange("p (n u) -> p n u", u=2),
+                in_=x_turned[j][:].rearrange("p u n -> p n u"),
             )
 
-        def quantise_x(blk):
-            x_codes[blk] = work.tile([P, HALF], U32, name="x_codes", align_bytes=64)
-            x_scales[blk] = work.tile([P, HALF], U8, name="x_scales", align_bytes=64)
+        def quantise_x(j):
+            blk, a = divmod(j, ROW_TILES)
+            if a == 0:
+                x_codes[blk] = work.tile([P, HALF], U32, name="x_codes", bufs=3, align_bytes=64)
+                x_scales[blk] = work.tile([P, HALF], U8, name="x_scales", bufs=3, align_bytes=64)
+            cols = slice(a * P, (a + 1) * P)
             nc.vector.quantize_mx(
-                out=x_codes[blk][:].bitcast(FP8X4), scales=x_scales[blk][:], in_=x_grouped[blk][:]
+                out=x_codes[blk][:, cols].bitcast(FP8X4), scales=x_scales[blk][:, cols], in_=x_grouped[j][:]
             )
 
         def where(t):
             blk, ot = divmod(t, OUT_TILES)
-            return blk, ot, blk // (ROWS // HALF)
+            return blk, ot, blk // HALVES
 
         def coef(table, width, g, i):
             return table[:, width * g + i : width * g + i + 1]
@@ -97,14 +101,14 @@ def tile_groupkanlayer_e_kernel(tc, x, W_words, W_scales, b, p, q, out):
         def add_bias(t):
             blk, ot, g = where(t)
             nc.scalar.activation(
-                out=chain_tile(y_sb, t, "y", 3)[:], in_=s_ps[t][:], func=ACT.Identity,
+                out=chain_tile(y_sb, t, "y", 4)[:], in_=s_ps[t][:], func=ACT.Identity,
                 bias=coef(b_cols, OUT_TILES, g, ot), scale=1.0,
             )
 
         def den_linear(t):
             g = where(t)[2]
             nc.scalar.activation(
-                out=chain_tile(d1_sb, t, "d1", 3)[:], in_=y_sb[t][:], func=ACT.Identity,
+                out=chain_tile(d1_sb, t, "d1", 4)[:], in_=y_sb[t][:], func=ACT.Identity,
                 bias=coef(q_f32, 3, g, 1), scale=coef(q_f32, 3, g, 2),
             )
 
@@ -131,20 +135,35 @@ def tile_groupkanlayer_e_kernel(tc, x, W_words, W_scales, b, p, q, out):
             for a in range(ROW_TILES):
                 nc.tensor.transpose(dst[t][:, a, :], src[t][:, a * P : (a + 1) * P], ident[:])
 
+        def absolute(t):
+            nc.scalar.activation(
+                out=chain_tile(a_sb, t, "a", 2)[:], in_=den_ps[t][:].rearrange("p a o -> p (a o)"),
+                func=ACT.Abs,
+            )
+
+        def root_of_reciprocal(t):
+            nc.scalar.activation(
+                out=chain_tile(u_sb, t, "u", 2)[:], in_=a_sb[t][:], func=ACT.Abs_reciprocal_sqrt,
+                bias=one[:, 0:1], scale=1.0,
+            )
+
+        def reciprocal(t):
+            nc.scalar.activation(out=chain_tile(r_sb, t, "r", 4)[:], in_=u_sb[t][:], func=ACT.Square)
+
         def finish(t):
             blk, ot, g = where(t)
-            if ot == 0:
-                stage[blk] = work.tile([P, ROW_TILES, GOUT], F32, name="stage", bufs=3)
+            out_sb = work.tile([P, ROW_TILES, P], F32, name="out_sb", bufs=3)
             nc.vector.scalar_tensor_tensor(
-                out=stage[blk][:, :, ot * P : (ot + 1) * P], in0=num_ps[t][:], scalar=coef(p_f32, 4, g, 0),
+                out=out_sb[:], in0=num_ps[t][:], scalar=coef(p_f32, 4, g, 0),
                 in1=r_sb[t][:].rearrange("p (a o) -> p a o", a=ROW_TILES), op0=ALU.add, op1=ALU.mult,
             )
-            if ot == OUT_TILES - 1:
-                half = blk % (ROWS // HALF)
-                rows = out[half * HALF : (half + 1) * HALF, g * GOUT : (g + 1) * GOUT]
-                nc.sync.dma_start(out=rows.rearrange("(a r) o -> r a o", r=P), in_=stage[blk][:])
+            row0, col0 = blk % HALVES * HALF, g * GOUT + ot * P
+            nc.sync.dma_start(
+                out=out[row0 : row0 + HALF, col0 : col0 + P].rearrange("(a r) o -> r a o", r=P), in_=out_sb[:]
+            )
 
-        load_x(0)
+        for j in range(ROW_TILES):
+            load_x(j)
 
         w_planes = const.tile([P, GROUPS, GOUT], U8, align_bytes=64)
         nc.vector.memset(w_planes[:].bitcast(I32), 0)
@@ -160,7 +179,8 @@ def tile_groupkanlayer_e_kernel(tc, x, W_words, W_scales, b, p, q, out):
         w_words = const.tile([P, GROUPS, 2 * GOUT], U8, align_bytes=64)
         w_dram = W_words.bitcast(I32).rearrange("g pp w -> pp g w")
         nc.sync.dma_start(out=w_words[:, 0:1, :].bitcast(I32), in_=w_dram[:, 0:1, :])
-        load_x(1)
+        for j in range(ROW_TILES, AT_TURN_X - AT_LOAD):
+            load_x(j)
         nc.sync.dma_start(out=w_words[:, 1:GROUPS, :].bitcast(I32), in_=w_dram[:, 1:GROUPS, :])
 
         ident = const.tile([P, P], F32)
@@ -185,56 +205,50 @@ def tile_groupkanlayer_e_kernel(tc, x, W_words, W_scales, b, p, q, out):
         b_cols = const.tile([P, GROUPS * OUT_TILES], F32)
         nc.vector.tensor_copy(out=b_cols[:], in_=b_turned[:, 0 : GROUPS * OUT_TILES])
 
-        def live(t):
-            return 0 <= t < TILES
+        def due(step, at, count):
+            t = step - at
+            return t if 0 <= t < count else None
 
-        for step in range(-OUT_TILES, TILES + 4):
-            next_blk, phase = step // OUT_TILES + 1, step % OUT_TILES
-            prepare = next_blk < BLOCKS
-            t_in, t_poly, t_den, t_num, t_out = step, step - 1, step - 2, step - 3, step - 4
+        for step in range(AT_TURN_X, TILES + AT_FINISH):
+            j = due(step, AT_LOAD, PIECES)
+            if j is not None:
+                load_x(j)
 
-            if phase == 0 and next_blk + 2 < BLOCKS:
-                load_x(next_blk + 2)
-
-            if phase == 3 and prepare:
-                quantise_x(next_blk)
-            if live(t_poly):
-                g = where(t_poly)[2]
-                num_linear(t_poly)
-                times_y(d2_sb, d1_sb, t_poly, "d2")
-            if live(t_out):
+            j, t, t_out = due(step, AT_QUANTISE, PIECES), due(step, AT_POLY, TILES), due(step, AT_FINISH, TILES)
+            if j is not None:
+                quantise_x(j)
+            if t is not None:
+                g = where(t)[2]
+                num_linear(t)
+                times_y(d2_sb, d1_sb, t, "d2")
+            if t_out is not None:
                 finish(t_out)
-            if live(t_poly):
-                times_y(n2_sb, n1_sb, t_poly, "n2")
-                plus_times_y(d3_sb, d2_sb, t_poly, "d3", 3, coef(q_f32, 3, g, 0))
-                plus_times_y(n3_sb, n2_sb, t_poly, "n3", 4, coef(p_f32, 4, g, 1))
+            if t is not None:
+                times_y(n2_sb, n1_sb, t, "n2")
+                plus_times_y(d3_sb, d2_sb, t, "d3", 4, coef(q_f32, 3, g, 0))
+                plus_times_y(n3_sb, n2_sb, t, "n3", 6, coef(p_f32, 4, g, 1))
 
-            if live(t_num):
-                nc.scalar.activation(
-                    out=chain_tile(a_sb, t_num, "a", 2)[:],
-                    in_=den_ps[t_num][:].rearrange("p a o -> p (a o)"), func=ACT.Abs,
-                )
-            if live(t_in):
-                add_bias(t_in)
-            if live(t_num):
-                nc.scalar.activation(
-                    out=chain_tile(u_sb, t_num, "u", 2)[:], in_=a_sb[t_num][:],
-                    func=ACT.Abs_reciprocal_sqrt, bias=one[:, 0:1], scale=1.0,
-                )
-            if live(t_in):
-                den_linear(t_in)
-            if live(t_num):
-                nc.scalar.activation(
-                    out=chain_tile(r_sb, t_num, "r", 3)[:], in_=u_sb[t_num][:], func=ACT.Square
-                )
-            if phase in (1, 2) and prepare:
-                group_x(next_blk, phase - 1)
+            j, t, t_rec = due(step, AT_GROUP_X, PIECES), due(step, AT_BIAS, TILES), due(step, AT_RECIPROCAL, TILES)
+            if t_rec is not None:
+                absolute(t_rec)
+            if t is not None:
+                add_bias(t)
+            if t_rec is not None:
+                root_of_reciprocal(t_rec)
+            if t is not None:
+                den_linear(t)
+            if t_rec is not None:
+                reciprocal(t_rec)
+            if j is not None:
+                group_x(j)
 
-            if live(t_den):
+            t_den, t_num = due(step, AT_TURN_DEN, TILES), due(step, AT_TURN_NUM, TILES)
+            j, t = due(step, AT_TURN_X, PIECES), due(step, AT_MULTIPLY, TILES)
+            if t_den is not None:
                 turn_back(den_ps, d3_sb, t_den, "den_ps")
-            if live(t_num):
+            if t_num is not None:
                 turn_back(num_ps, n3_sb, t_num, "num_ps")
-            if phase in (0, 1) and prepare:
-                turn_x(next_blk, phase)
-            if live(t_in + 1):
-                multiply(t_in + 1)
+            if j is not None:
+                turn_x(j)
+            if t is not None:
+                multiply(t)

@@ -27,7 +27,8 @@ TILES = BLOCKS * OUT_TILES
 PIECES = BLOCKS * ROW_TILES
 
 AT_LOAD, AT_TURN_X, AT_GROUP_X, AT_QUANTISE = -15, -7, -6, -5
-AT_MULTIPLY, AT_BIAS, AT_POLY, AT_TURN_DEN, AT_RECIPROCAL, AT_TURN_NUM, AT_FINISH = -1, 0, 2, 4, 5, 6, 7
+AT_MULTIPLY, AT_BIAS, AT_LINEAR, AT_PRODUCT_1, AT_PRODUCT_2, AT_TURN_DEN = -1, 0, 0, 1, 2, 3
+AT_ABS, AT_ROOT, AT_SQUARE, AT_TURN_NUM, AT_FINISH = 4, 5, 6, 6, 7
 
 FLOPS = 2 * ROWS * GROUPS * GIN * GOUT
 
@@ -53,7 +54,7 @@ def tile_groupkanlayer_e_kernel(tc, x, W_words, W_scales, b, p, q, out):
 
         def turn_x(j):
             words = x_rows[j][:].bitcast(F32)
-            x_turned[j] = psum.tile([P, 2, P], F32, name="x_turned")
+            x_turned[j] = psum.tile([P, 2, P], F32, name="x_turned", bufs=1)
             for u in range(2):
                 nc.tensor.transpose(x_turned[j][:, u, :], words[:, u : GIN // 2 : 2], ident[:])
 
@@ -87,7 +88,7 @@ def tile_groupkanlayer_e_kernel(tc, x, W_words, W_scales, b, p, q, out):
 
         def multiply(t):
             blk, ot, g = where(t)
-            s_ps[t] = psum.tile([P, HALF], F32, name="s_ps")
+            s_ps[t] = psum.tile([P, HALF], F32, name="s_ps", bufs=3)
             nc.tensor.matmul_mx(
                 out=s_ps[t][:],
                 lhsT=w_words[:, g, 2 * P * ot : 2 * P * (ot + 1)].bitcast(FP4X4),
@@ -105,23 +106,17 @@ def tile_groupkanlayer_e_kernel(tc, x, W_words, W_scales, b, p, q, out):
                 bias=coef(b_cols, OUT_TILES, g, ot), scale=1.0,
             )
 
-        def den_linear(t):
-            g = where(t)[2]
-            nc.scalar.activation(
-                out=chain_tile(d1_sb, t, "d1", 4)[:], in_=y_sb[t][:], func=ACT.Identity,
-                bias=coef(q_f32, 3, g, 1), scale=coef(q_f32, 3, g, 2),
-            )
-
-        def num_linear(t):
-            g = where(t)[2]
-            nc.vector.tensor_scalar(
-                out=chain_tile(n1_sb, t, "n1", 2)[:], in0=y_sb[t][:],
-                scalar1=coef(p_f32, 4, g, 3), scalar2=coef(p_f32, 4, g, 2), op0=ALU.mult, op1=ALU.add,
+        def linear(dst, t, name, slope, offset):
+            nc.gpsimd.tensor_scalar(
+                out=chain_tile(dst, t, name, 3)[:], in0=y_sb[t][:],
+                scalar1=slope, scalar2=offset, op0=ALU.mult, op1=ALU.add,
             )
 
         def times_y(dst, src, t, name):
-            nc.vector.tensor_tensor(
-                out=chain_tile(dst, t, name, 2)[:], in0=src[t][:], in1=y_sb[t][:], op=ALU.mult
+            blk, ot, g = where(t)
+            nc.vector.scalar_tensor_tensor(
+                out=chain_tile(dst, t, name, 3)[:], in0=s_ps[t][:], scalar=coef(b_cols, OUT_TILES, g, ot),
+                in1=src[t][:], op0=ALU.add, op1=ALU.mult,
             )
 
         def plus_times_y(dst, src, t, name, bufs, c):
@@ -137,13 +132,13 @@ def tile_groupkanlayer_e_kernel(tc, x, W_words, W_scales, b, p, q, out):
 
         def absolute(t):
             nc.scalar.activation(
-                out=chain_tile(a_sb, t, "a", 2)[:], in_=den_ps[t][:].rearrange("p a o -> p (a o)"),
+                out=chain_tile(a_sb, t, "a", 3)[:], in_=den_ps[t][:].rearrange("p a o -> p (a o)"),
                 func=ACT.Abs,
             )
 
         def root_of_reciprocal(t):
             nc.scalar.activation(
-                out=chain_tile(u_sb, t, "u", 2)[:], in_=a_sb[t][:], func=ACT.Abs_reciprocal_sqrt,
+                out=chain_tile(u_sb, t, "u", 3)[:], in_=a_sb[t][:], func=ACT.Abs_reciprocal_sqrt,
                 bias=one[:, 0:1], scale=1.0,
             )
 
@@ -200,7 +195,7 @@ def tile_groupkanlayer_e_kernel(tc, x, W_words, W_scales, b, p, q, out):
         )
         b_rows_f32 = const.tile([P, P], F32)
         nc.vector.tensor_copy(out=b_rows_f32[:], in_=b_rows[:])
-        b_turned = psum.tile([P, HALF], F32, name="s_ps")
+        b_turned = psum.tile([P, HALF], F32, name="s_ps", bufs=3)
         nc.tensor.transpose(b_turned[:, 0:P], b_rows_f32[:], ident[:])
         b_cols = const.tile([P, GROUPS * OUT_TILES], F32)
         nc.vector.tensor_copy(out=b_cols[:], in_=b_turned[:, 0 : GROUPS * OUT_TILES])
@@ -214,33 +209,38 @@ def tile_groupkanlayer_e_kernel(tc, x, W_words, W_scales, b, p, q, out):
             if j is not None:
                 load_x(j)
 
-            j, t, t_out = due(step, AT_QUANTISE, PIECES), due(step, AT_POLY, TILES), due(step, AT_FINISH, TILES)
+            j = due(step, AT_QUANTISE, PIECES)
+            t1, t2, t_out = due(step, AT_PRODUCT_1, TILES), due(step, AT_PRODUCT_2, TILES), due(step, AT_FINISH, TILES)
             if j is not None:
                 quantise_x(j)
-            if t is not None:
-                g = where(t)[2]
-                num_linear(t)
-                times_y(d2_sb, d1_sb, t, "d2")
+            if t2 is not None:
+                g = where(t2)[2]
+                plus_times_y(d3_sb, d2_sb, t2, "d3", 3, coef(q_f32, 3, g, 0))
+                plus_times_y(n3_sb, n2_sb, t2, "n3", 6, coef(p_f32, 4, g, 1))
+            if t1 is not None:
+                times_y(d2_sb, d1_sb, t1, "d2")
+                times_y(n2_sb, n1_sb, t1, "n2")
             if t_out is not None:
                 finish(t_out)
-            if t is not None:
-                times_y(n2_sb, n1_sb, t, "n2")
-                plus_times_y(d3_sb, d2_sb, t, "d3", 4, coef(q_f32, 3, g, 0))
-                plus_times_y(n3_sb, n2_sb, t, "n3", 6, coef(p_f32, 4, g, 1))
 
-            j, t, t_rec = due(step, AT_GROUP_X, PIECES), due(step, AT_BIAS, TILES), due(step, AT_RECIPROCAL, TILES)
-            if t_rec is not None:
-                absolute(t_rec)
-            if t is not None:
-                add_bias(t)
-            if t_rec is not None:
-                root_of_reciprocal(t_rec)
-            if t is not None:
-                den_linear(t)
-            if t_rec is not None:
-                reciprocal(t_rec)
+            j, t = due(step, AT_GROUP_X, PIECES), due(step, AT_BIAS, TILES)
+            t_abs, t_root, t_square = due(step, AT_ABS, TILES), due(step, AT_ROOT, TILES), due(step, AT_SQUARE, TILES)
             if j is not None:
                 group_x(j)
+            if t is not None:
+                add_bias(t)
+            if t_abs is not None:
+                absolute(t_abs)
+            if t_root is not None:
+                root_of_reciprocal(t_root)
+            if t_square is not None:
+                reciprocal(t_square)
+
+            t = due(step, AT_LINEAR, TILES)
+            if t is not None:
+                g = where(t)[2]
+                linear(d1_sb, t, "d1", coef(q_f32, 3, g, 2), coef(q_f32, 3, g, 1))
+                linear(n1_sb, t, "n1", coef(p_f32, 4, g, 3), coef(p_f32, 4, g, 2))
 
             t_den, t_num = due(step, AT_TURN_DEN, TILES), due(step, AT_TURN_NUM, TILES)
             j, t = due(step, AT_TURN_X, PIECES), due(step, AT_MULTIPLY, TILES)
@@ -248,7 +248,7 @@ def tile_groupkanlayer_e_kernel(tc, x, W_words, W_scales, b, p, q, out):
                 turn_back(den_ps, d3_sb, t_den, "den_ps")
             if t_num is not None:
                 turn_back(num_ps, n3_sb, t_num, "num_ps")
-            if j is not None:
-                turn_x(j)
             if t is not None:
                 multiply(t)
+            if j is not None:
+                turn_x(j)

@@ -25,6 +25,7 @@ OUT_TILES = GOUT // P
 BLOCKS = GROUPS * HALVES
 TILES = BLOCKS * OUT_TILES
 PIECES = BLOCKS * ROW_TILES
+DEN, NUM = 0, 1
 
 AT_LOAD, AT_TURN_X, AT_GROUP_X, AT_QUANTISE = -15, -7, -6, -5
 AT_MULTIPLY, AT_BIAS, AT_LINEAR, AT_PRODUCT_1, AT_PRODUCT_2, AT_TURN_DEN = -1, 0, 0, 1, 2, 3
@@ -42,7 +43,7 @@ def tile_groupkanlayer_e_kernel(tc, x, W_words, W_scales, b, p, q, out):
         ctx.enter_context(tc.manual_schedule())
 
         x_rows, x_turned, x_grouped, x_codes, x_scales = {}, {}, {}, {}, {}
-        s_ps, y_sb, n1_sb, d1_sb, n2_sb, d2_sb, n3_sb, d3_sb = {}, {}, {}, {}, {}, {}, {}, {}
+        s_ps, y_sb, lin_sb, quad_sb, n3_sb, d3_sb = {}, {}, {}, {}, {}, {}
         num_ps, den_ps, a_sb, u_sb, r_sb = {}, {}, {}, {}, {}
 
         def load_x(j):
@@ -59,20 +60,19 @@ def tile_groupkanlayer_e_kernel(tc, x, W_words, W_scales, b, p, q, out):
                 nc.tensor.transpose(x_turned[j][:, u, :], words[:, u : GIN // 2 : 2], ident[:])
 
         def group_x(j):
-            x_grouped[j] = work.tile([P, 4 * P], BF16, name="x_grouped", bufs=3, align_bytes=64)
+            blk, a = divmod(j, ROW_TILES)
+            if a == 0:
+                x_grouped[blk] = work.tile([P, 4 * HALF], BF16, name="x_grouped", bufs=3, align_bytes=64)
             nc.scalar.copy(
-                out=x_grouped[j][:].bitcast(F32).rearrange("p (n u) -> p n u", u=2),
+                out=x_grouped[blk][:, 4 * P * a : 4 * P * (a + 1)].bitcast(F32).rearrange("p (n u) -> p n u", u=2),
                 in_=x_turned[j][:].rearrange("p u n -> p n u"),
             )
 
-        def quantise_x(j):
-            blk, a = divmod(j, ROW_TILES)
-            if a == 0:
-                x_codes[blk] = work.tile([P, HALF], U32, name="x_codes", bufs=3, align_bytes=64)
-                x_scales[blk] = work.tile([P, HALF], U8, name="x_scales", bufs=3, align_bytes=64)
-            cols = slice(a * P, (a + 1) * P)
+        def quantise_x(blk):
+            x_codes[blk] = work.tile([P, HALF], U32, name="x_codes", bufs=3, align_bytes=64)
+            x_scales[blk] = work.tile([P, HALF], U8, name="x_scales", bufs=3, align_bytes=64)
             nc.vector.quantize_mx(
-                out=x_codes[blk][:, cols].bitcast(FP8X4), scales=x_scales[blk][:, cols], in_=x_grouped[j][:]
+                out=x_codes[blk][:].bitcast(FP8X4), scales=x_scales[blk][:], in_=x_grouped[blk][:]
             )
 
         def where(t):
@@ -106,22 +106,29 @@ def tile_groupkanlayer_e_kernel(tc, x, W_words, W_scales, b, p, q, out):
                 bias=coef(b_cols, OUT_TILES, g, ot), scale=1.0,
             )
 
-        def linear(dst, t, name, slope, offset):
+        def linear(t):
+            g = where(t)[2]
+            lin_sb[t] = work.tile([P, 2, HALF], F32, name="lin", bufs=3)
             nc.gpsimd.tensor_scalar(
-                out=chain_tile(dst, t, name, 3)[:], in0=y_sb[t][:],
-                scalar1=slope, scalar2=offset, op0=ALU.mult, op1=ALU.add,
+                out=lin_sb[t][:, DEN, :], in0=y_sb[t][:],
+                scalar1=coef(q_f32, 3, g, 2), scalar2=coef(q_f32, 3, g, 1), op0=ALU.mult, op1=ALU.add,
+            )
+            nc.gpsimd.tensor_scalar(
+                out=lin_sb[t][:, NUM, :], in0=y_sb[t][:],
+                scalar1=coef(p_f32, 4, g, 3), scalar2=coef(p_f32, 4, g, 2), op0=ALU.mult, op1=ALU.add,
             )
 
-        def times_y(dst, src, t, name):
+        def times_y(t):
             blk, ot, g = where(t)
+            quad_sb[t] = work.tile([P, 2, HALF], F32, name="quad", bufs=3)
             nc.vector.scalar_tensor_tensor(
-                out=chain_tile(dst, t, name, 3)[:], in0=s_ps[t][:], scalar=coef(b_cols, OUT_TILES, g, ot),
-                in1=src[t][:], op0=ALU.add, op1=ALU.mult,
+                out=quad_sb[t][:], in0=s_ps[t][:].unsqueeze(1).to_broadcast([P, 2, HALF]),
+                scalar=coef(b_cols, OUT_TILES, g, ot), in1=lin_sb[t][:], op0=ALU.add, op1=ALU.mult,
             )
 
-        def plus_times_y(dst, src, t, name, bufs, c):
+        def plus_times_y(dst, plane, t, name, bufs, c):
             nc.vector.scalar_tensor_tensor(
-                out=chain_tile(dst, t, name, bufs)[:], in0=src[t][:], scalar=c, in1=y_sb[t][:],
+                out=chain_tile(dst, t, name, bufs)[:], in0=quad_sb[t][:, plane, :], scalar=c, in1=y_sb[t][:],
                 op0=ALU.add, op1=ALU.mult,
             )
 
@@ -160,12 +167,15 @@ def tile_groupkanlayer_e_kernel(tc, x, W_words, W_scales, b, p, q, out):
         for j in range(ROW_TILES):
             load_x(j)
 
+        b_bf = const.tile([GROUPS * OUT_TILES, P], BF16)
+        nc.scalar.dma_start(out=b_bf[:], in_=b.rearrange("g (ot o) -> (g ot) o", o=P))
+        b_rows = const.tile([P, P], F32)
+        nc.vector.memset(b_rows[:], 0.0)
+        ident = const.tile([P, P], F32)
+        make_identity(nc, ident[:])
+
         w_planes = const.tile([P, GROUPS, GOUT], U8, align_bytes=64)
         nc.vector.memset(w_planes[:].bitcast(I32), 0)
-        b_rows = const.tile([P, P], BF16)
-        nc.vector.memset(b_rows[:], 0.0)
-        one = const.tile([P, 1], F32)
-        nc.vector.memset(one[:], 1.0)
         for quad in range(4):
             nc.sync.dma_start(
                 out=w_planes[32 * quad : 32 * quad + 4].bitcast(I32),
@@ -178,27 +188,22 @@ def tile_groupkanlayer_e_kernel(tc, x, W_words, W_scales, b, p, q, out):
             load_x(j)
         nc.sync.dma_start(out=w_words[:, 1:GROUPS, :].bitcast(I32), in_=w_dram[:, 1:GROUPS, :])
 
-        ident = const.tile([P, P], F32)
-        make_identity(nc, ident[:])
-
         p_bf = const.tile([P, GROUPS * 4], BF16)
         q_bf = const.tile([P, GROUPS * 3], BF16)
         nc.scalar.dma_start(out=p_bf[:], in_=p.rearrange("g c -> (g c)").partition_broadcast(P))
         nc.scalar.dma_start(out=q_bf[:], in_=q.rearrange("g c -> (g c)").partition_broadcast(P))
+        one = const.tile([P, 1], F32)
+        nc.vector.memset(one[:], 1.0)
+
+        nc.vector.tensor_copy(out=b_rows[0 : GROUPS * OUT_TILES, :], in_=b_bf[:])
+        b_turned = psum.tile([P, HALF], F32, name="s_ps", bufs=3)
+        nc.tensor.transpose(b_turned[:, 0:P], b_rows[:], ident[:])
+        b_cols = const.tile([P, GROUPS * OUT_TILES], F32)
+        nc.vector.tensor_copy(out=b_cols[:], in_=b_turned[:, 0 : GROUPS * OUT_TILES])
         p_f32 = const.tile([P, GROUPS * 4], F32)
         q_f32 = const.tile([P, GROUPS * 3], F32)
         nc.vector.tensor_copy(out=p_f32[:], in_=p_bf[:])
         nc.vector.tensor_copy(out=q_f32[:], in_=q_bf[:])
-
-        nc.scalar.dma_start(
-            out=b_rows[0 : GROUPS * OUT_TILES, :], in_=b.rearrange("g (ot o) -> (g ot) o", o=P)
-        )
-        b_rows_f32 = const.tile([P, P], F32)
-        nc.vector.tensor_copy(out=b_rows_f32[:], in_=b_rows[:])
-        b_turned = psum.tile([P, HALF], F32, name="s_ps", bufs=3)
-        nc.tensor.transpose(b_turned[:, 0:P], b_rows_f32[:], ident[:])
-        b_cols = const.tile([P, GROUPS * OUT_TILES], F32)
-        nc.vector.tensor_copy(out=b_cols[:], in_=b_turned[:, 0 : GROUPS * OUT_TILES])
 
         def due(step, at, count):
             t = step - at
@@ -211,15 +216,14 @@ def tile_groupkanlayer_e_kernel(tc, x, W_words, W_scales, b, p, q, out):
 
             j = due(step, AT_QUANTISE, PIECES)
             t1, t2, t_out = due(step, AT_PRODUCT_1, TILES), due(step, AT_PRODUCT_2, TILES), due(step, AT_FINISH, TILES)
-            if j is not None:
-                quantise_x(j)
+            if j is not None and j % ROW_TILES == ROW_TILES - 1:
+                quantise_x(j // ROW_TILES)
             if t2 is not None:
                 g = where(t2)[2]
-                plus_times_y(d3_sb, d2_sb, t2, "d3", 3, coef(q_f32, 3, g, 0))
-                plus_times_y(n3_sb, n2_sb, t2, "n3", 6, coef(p_f32, 4, g, 1))
+                plus_times_y(d3_sb, DEN, t2, "d3", 3, coef(q_f32, 3, g, 0))
+                plus_times_y(n3_sb, NUM, t2, "n3", 6, coef(p_f32, 4, g, 1))
             if t1 is not None:
-                times_y(d2_sb, d1_sb, t1, "d2")
-                times_y(n2_sb, n1_sb, t1, "n2")
+                times_y(t1)
             if t_out is not None:
                 finish(t_out)
 
@@ -238,9 +242,7 @@ def tile_groupkanlayer_e_kernel(tc, x, W_words, W_scales, b, p, q, out):
 
             t = due(step, AT_LINEAR, TILES)
             if t is not None:
-                g = where(t)[2]
-                linear(d1_sb, t, "d1", coef(q_f32, 3, g, 2), coef(q_f32, 3, g, 1))
-                linear(n1_sb, t, "n1", coef(p_f32, 4, g, 3), coef(p_f32, 4, g, 2))
+                linear(t)
 
             t_den, t_num = due(step, AT_TURN_DEN, TILES), due(step, AT_TURN_NUM, TILES)
             j, t = due(step, AT_TURN_X, PIECES), due(step, AT_MULTIPLY, TILES)

@@ -22,16 +22,28 @@ HALF = 512
 HALVES = ROWS // HALF
 ROW_TILES = HALF // P
 OUT_TILES = GOUT // P
-BLOCKS = GROUPS * HALVES
-TILES = BLOCKS * OUT_TILES
-PIECES = BLOCKS * ROW_TILES
+PANELS = GROUPS * HALVES
+TILES = PANELS * OUT_TILES
+PIECES = PANELS * ROW_TILES
 DEN, NUM = 0, 1
+P_COEFS, Q_COEFS = 4, 3
 
 AT_LOAD, AT_TURN_X, AT_GROUP_X, AT_QUANTISE = -15, -7, -6, -5
-AT_MULTIPLY, AT_BIAS, AT_LINEAR, AT_PRODUCT_1, AT_PRODUCT_2, AT_TURN_DEN = -1, 0, 0, 1, 2, 3
+AT_MULTIPLY, AT_BIAS, AT_LINEAR, AT_QUAD, AT_CUBIC, AT_TURN_DEN = -1, 0, 0, 1, 2, 3
 AT_ABS, AT_ROOT, AT_SQUARE, AT_TURN_NUM, AT_FINISH = 4, 5, 6, 6, 7
 
+PANEL_BUFS = 2
+STORE_BUFS = 3
+
 FLOPS = 2 * ROWS * GROUPS * GIN * GOUT
+
+
+def sbuf_slots(at_write, at_last_read):
+    return at_last_read - at_write + 2
+
+
+def psum_banks(at_write, at_last_read):
+    return at_last_read - at_write + 1
 
 
 def tile_groupkanlayer_e_kernel(tc, x, W_words, W_scales, b, p, q, out):
@@ -43,125 +55,137 @@ def tile_groupkanlayer_e_kernel(tc, x, W_words, W_scales, b, p, q, out):
         ctx.enter_context(tc.manual_schedule())
 
         x_rows, x_turned, x_grouped, x_codes, x_scales = {}, {}, {}, {}, {}
-        s_ps, y_sb, lin_sb, quad_sb, n3_sb, d3_sb = {}, {}, {}, {}, {}, {}
-        num_ps, den_ps, a_sb, u_sb, r_sb = {}, {}, {}, {}, {}
+        s_ps, y_sb, lin_sb, quad_sb, den_sb, num_sb = {}, {}, {}, {}, {}, {}
+        den_ps, num_ps, a_sb, u_sb, r_sb = {}, {}, {}, {}, {}
 
         def load_x(j):
-            blk, a = divmod(j, ROW_TILES)
-            g, half = divmod(blk, HALVES)
-            row0 = half * HALF + a * P
-            x_rows[j] = work.tile([P, GIN], BF16, name="x_rows", bufs=AT_TURN_X - AT_LOAD + 2)
+            pan, rt = divmod(j, ROW_TILES)
+            g, half = divmod(pan, HALVES)
+            row0 = half * HALF + rt * P
+            x_rows[j] = work.tile([P, GIN], BF16, name="x_rows", bufs=sbuf_slots(AT_LOAD, AT_TURN_X))
             nc.sync.dma_start(out=x_rows[j][:], in_=x[row0 : row0 + P, g * GIN : (g + 1) * GIN])
 
         def turn_x(j):
             words = x_rows[j][:].bitcast(F32)
             x_turned[j] = psum.tile([P, 2, P], F32, name="x_turned", bufs=1)
-            for u in range(2):
-                nc.tensor.transpose(x_turned[j][:, u, :], words[:, u : GIN // 2 : 2], ident[:])
+            for w in range(2):
+                nc.tensor.transpose(x_turned[j][:, w, :], words[:, w : GIN // 2 : 2], ident[:])
 
         def group_x(j):
-            blk, a = divmod(j, ROW_TILES)
-            if a == 0:
-                x_grouped[blk] = work.tile([P, 4 * HALF], BF16, name="x_grouped", bufs=3, align_bytes=64)
+            pan, rt = divmod(j, ROW_TILES)
+            if rt == 0:
+                x_grouped[pan] = work.tile([P, 4 * HALF], BF16, name="x_grouped", bufs=PANEL_BUFS, align_bytes=64)
             nc.scalar.copy(
-                out=x_grouped[blk][:, 4 * P * a : 4 * P * (a + 1)].bitcast(F32).rearrange("p (n u) -> p n u", u=2),
-                in_=x_turned[j][:].rearrange("p u n -> p n u"),
+                out=x_grouped[pan][:, 4 * P * rt : 4 * P * (rt + 1)].bitcast(F32).rearrange("pp (n w) -> pp n w", w=2),
+                in_=x_turned[j][:].rearrange("pp w n -> pp n w"),
             )
 
-        def quantise_x(blk):
-            x_codes[blk] = work.tile([P, HALF], U32, name="x_codes", bufs=3, align_bytes=64)
-            x_scales[blk] = work.tile([P, HALF], U8, name="x_scales", bufs=3, align_bytes=64)
+        def quantise_x(pan):
+            x_codes[pan] = work.tile([P, HALF], U32, name="x_codes", bufs=PANEL_BUFS, align_bytes=64)
+            x_scales[pan] = work.tile([P, HALF], U8, name="x_scales", bufs=PANEL_BUFS, align_bytes=64)
             nc.vector.quantize_mx(
-                out=x_codes[blk][:].bitcast(FP8X4), scales=x_scales[blk][:], in_=x_grouped[blk][:]
+                out=x_codes[pan][:].bitcast(FP8X4), scales=x_scales[pan][:], in_=x_grouped[pan][:]
             )
 
         def where(t):
-            blk, ot = divmod(t, OUT_TILES)
-            return blk, ot, blk // HALVES
+            pan, ot = divmod(t, OUT_TILES)
+            return pan, ot, pan // HALVES
 
-        def coef(table, width, g, i):
+        def column(table, width, g, i):
             return table[:, width * g + i : width * g + i + 1]
 
-        def chain_tile(store, t, name, bufs):
-            store[t] = work.tile([P, HALF], F32, name=name, bufs=bufs)
-            return store[t]
-
         def multiply(t):
-            blk, ot, g = where(t)
-            s_ps[t] = psum.tile([P, HALF], F32, name="s_ps", bufs=3)
+            pan, ot, g = where(t)
+            s_ps[t] = psum.tile([P, HALF], F32, name="s_ps", bufs=psum_banks(AT_MULTIPLY, AT_QUAD))
             nc.tensor.matmul_mx(
                 out=s_ps[t][:],
                 lhsT=w_words[:, g, 2 * P * ot : 2 * P * (ot + 1)].bitcast(FP4X4),
-                lhsT_scale=w_planes[:, g, P * ot : P * (ot + 1)],
-                rhs=x_codes[blk][:].bitcast(FP8X4),
-                rhs_scale=x_scales[blk][:],
+                lhsT_scale=w_scales[:, g, P * ot : P * (ot + 1)],
+                rhs=x_codes[pan][:].bitcast(FP8X4),
+                rhs_scale=x_scales[pan][:],
                 start=True,
                 stop=True,
             )
 
         def add_bias(t):
-            blk, ot, g = where(t)
+            pan, ot, g = where(t)
+            y_sb[t] = work.tile([P, HALF], F32, name="y", bufs=sbuf_slots(AT_BIAS, AT_CUBIC))
             nc.scalar.activation(
-                out=chain_tile(y_sb, t, "y", 4)[:], in_=s_ps[t][:], func=ACT.Identity,
-                bias=coef(b_cols, OUT_TILES, g, ot), scale=1.0,
+                out=y_sb[t][:], in_=s_ps[t][:], func=ACT.Identity,
+                bias=column(b_cols, OUT_TILES, g, ot), scale=1.0,
             )
 
         def linear(t):
             g = where(t)[2]
-            lin_sb[t] = work.tile([P, 2, HALF], F32, name="lin", bufs=3)
+            lin_sb[t] = work.tile([P, 2, HALF], F32, name="lin", bufs=sbuf_slots(AT_LINEAR, AT_QUAD))
             nc.gpsimd.tensor_scalar(
                 out=lin_sb[t][:, DEN, :], in0=y_sb[t][:],
-                scalar1=coef(q_f32, 3, g, 2), scalar2=coef(q_f32, 3, g, 1), op0=ALU.mult, op1=ALU.add,
+                scalar1=column(q_f32, Q_COEFS, g, 2), scalar2=column(q_f32, Q_COEFS, g, 1),
+                op0=ALU.mult, op1=ALU.add,
             )
             nc.gpsimd.tensor_scalar(
                 out=lin_sb[t][:, NUM, :], in0=y_sb[t][:],
-                scalar1=coef(p_f32, 4, g, 3), scalar2=coef(p_f32, 4, g, 2), op0=ALU.mult, op1=ALU.add,
+                scalar1=column(p_f32, P_COEFS, g, 3), scalar2=column(p_f32, P_COEFS, g, 2),
+                op0=ALU.mult, op1=ALU.add,
             )
 
-        def times_y(t):
-            blk, ot, g = where(t)
-            quad_sb[t] = work.tile([P, 2, HALF], F32, name="quad", bufs=3)
+        def quadratic(t):
+            pan, ot, g = where(t)
+            quad_sb[t] = work.tile([P, 2, HALF], F32, name="quad", bufs=sbuf_slots(AT_QUAD, AT_CUBIC))
             nc.vector.scalar_tensor_tensor(
                 out=quad_sb[t][:], in0=s_ps[t][:].unsqueeze(1).to_broadcast([P, 2, HALF]),
-                scalar=coef(b_cols, OUT_TILES, g, ot), in1=lin_sb[t][:], op0=ALU.add, op1=ALU.mult,
+                scalar=column(b_cols, OUT_TILES, g, ot), in1=lin_sb[t][:], op0=ALU.add, op1=ALU.mult,
             )
 
-        def plus_times_y(dst, plane, t, name, bufs, c):
+        def cubic(t):
+            g = where(t)[2]
+            den_sb[t] = work.tile([P, HALF], F32, name="den", bufs=sbuf_slots(AT_CUBIC, AT_TURN_DEN))
             nc.vector.scalar_tensor_tensor(
-                out=chain_tile(dst, t, name, bufs)[:], in0=quad_sb[t][:, plane, :], scalar=c, in1=y_sb[t][:],
-                op0=ALU.add, op1=ALU.mult,
+                out=den_sb[t][:], in0=quad_sb[t][:, DEN, :], scalar=column(q_f32, Q_COEFS, g, 0),
+                in1=y_sb[t][:], op0=ALU.add, op1=ALU.mult,
+            )
+            num_sb[t] = work.tile([P, HALF], F32, name="num", bufs=sbuf_slots(AT_CUBIC, AT_TURN_NUM))
+            nc.vector.scalar_tensor_tensor(
+                out=num_sb[t][:], in0=quad_sb[t][:, NUM, :], scalar=column(p_f32, P_COEFS, g, 1),
+                in1=y_sb[t][:], op0=ALU.add, op1=ALU.mult,
             )
 
-        def turn_back(dst, src, t, name):
-            dst[t] = psum.tile([P, ROW_TILES, P], F32, name=name)
-            for a in range(ROW_TILES):
-                nc.tensor.transpose(dst[t][:, a, :], src[t][:, a * P : (a + 1) * P], ident[:])
+        def turn_back(turned, src):
+            for rt in range(ROW_TILES):
+                nc.tensor.transpose(turned[:, rt, :], src[:, rt * P : (rt + 1) * P], ident[:])
+
+        def turn_den(t):
+            den_ps[t] = psum.tile([P, ROW_TILES, P], F32, name="den_ps", bufs=psum_banks(AT_TURN_DEN, AT_ABS))
+            turn_back(den_ps[t], den_sb[t])
+
+        def turn_num(t):
+            num_ps[t] = psum.tile([P, ROW_TILES, P], F32, name="num_ps", bufs=psum_banks(AT_TURN_NUM, AT_FINISH))
+            turn_back(num_ps[t], num_sb[t])
 
         def absolute(t):
+            a_sb[t] = work.tile([P, ROW_TILES, P], F32, name="a", bufs=sbuf_slots(AT_ABS, AT_ROOT))
+            nc.scalar.activation(out=a_sb[t][:], in_=den_ps[t][:], func=ACT.Abs)
+
+        def root(t):
+            u_sb[t] = work.tile([P, ROW_TILES, P], F32, name="u", bufs=sbuf_slots(AT_ROOT, AT_SQUARE))
             nc.scalar.activation(
-                out=chain_tile(a_sb, t, "a", 3)[:], in_=den_ps[t][:].rearrange("p a o -> p (a o)"),
-                func=ACT.Abs,
+                out=u_sb[t][:], in_=a_sb[t][:], func=ACT.Abs_reciprocal_sqrt, bias=one[:, 0:1], scale=1.0
             )
 
-        def root_of_reciprocal(t):
-            nc.scalar.activation(
-                out=chain_tile(u_sb, t, "u", 3)[:], in_=a_sb[t][:], func=ACT.Abs_reciprocal_sqrt,
-                bias=one[:, 0:1], scale=1.0,
-            )
-
-        def reciprocal(t):
-            nc.scalar.activation(out=chain_tile(r_sb, t, "r", 4)[:], in_=u_sb[t][:], func=ACT.Square)
+        def square(t):
+            r_sb[t] = work.tile([P, ROW_TILES, P], F32, name="r", bufs=sbuf_slots(AT_SQUARE, AT_FINISH))
+            nc.scalar.activation(out=r_sb[t][:], in_=u_sb[t][:], func=ACT.Square)
 
         def finish(t):
-            blk, ot, g = where(t)
-            out_sb = work.tile([P, ROW_TILES, P], F32, name="out_sb", bufs=3)
+            pan, ot, g = where(t)
+            out_sb = work.tile([P, ROW_TILES, P], F32, name="out_sb", bufs=STORE_BUFS)
             nc.vector.scalar_tensor_tensor(
-                out=out_sb[:], in0=num_ps[t][:], scalar=coef(p_f32, 4, g, 0),
-                in1=r_sb[t][:].rearrange("p (a o) -> p a o", a=ROW_TILES), op0=ALU.add, op1=ALU.mult,
+                out=out_sb[:], in0=num_ps[t][:], scalar=column(p_f32, P_COEFS, g, 0), in1=r_sb[t][:],
+                op0=ALU.add, op1=ALU.mult,
             )
-            row0, col0 = blk % HALVES * HALF, g * GOUT + ot * P
+            row0, col0 = pan % HALVES * HALF, g * GOUT + ot * P
             nc.sync.dma_start(
-                out=out[row0 : row0 + HALF, col0 : col0 + P].rearrange("(a r) o -> r a o", r=P), in_=out_sb[:]
+                out=out[row0 : row0 + HALF, col0 : col0 + P].rearrange("(rt n) o -> n rt o", n=P), in_=out_sb[:]
             )
 
         for j in range(ROW_TILES):
@@ -174,83 +198,62 @@ def tile_groupkanlayer_e_kernel(tc, x, W_words, W_scales, b, p, q, out):
         ident = const.tile([P, P], F32)
         make_identity(nc, ident[:])
 
-        w_planes = const.tile([P, GROUPS, GOUT], U8, align_bytes=64)
-        nc.vector.memset(w_planes[:].bitcast(I32), 0)
-        for quad in range(4):
+        w_scales = const.tile([P, GROUPS, GOUT], U8, align_bytes=64)
+        nc.vector.memset(w_scales[:].bitcast(I32), 0)
+        for c in range(4):
             nc.sync.dma_start(
-                out=w_planes[32 * quad : 32 * quad + 4].bitcast(I32),
-                in_=W_scales.bitcast(I32)[:, 4 * quad : 4 * quad + 4, :].rearrange("g r n -> r g n"),
+                out=w_scales[32 * c : 32 * c + 4].bitcast(I32),
+                in_=W_scales.bitcast(I32)[:, 4 * c : 4 * c + 4, :].rearrange("g i o -> i g o"),
             )
         w_words = const.tile([P, GROUPS, 2 * GOUT], U8, align_bytes=64)
-        w_dram = W_words.bitcast(I32).rearrange("g pp w -> pp g w")
+        w_dram = W_words.bitcast(I32).rearrange("g pp o -> pp g o")
         nc.sync.dma_start(out=w_words[:, 0:1, :].bitcast(I32), in_=w_dram[:, 0:1, :])
         for j in range(ROW_TILES, AT_TURN_X - AT_LOAD):
             load_x(j)
         nc.sync.dma_start(out=w_words[:, 1:GROUPS, :].bitcast(I32), in_=w_dram[:, 1:GROUPS, :])
 
-        p_bf = const.tile([P, GROUPS * 4], BF16)
-        q_bf = const.tile([P, GROUPS * 3], BF16)
-        nc.scalar.dma_start(out=p_bf[:], in_=p.rearrange("g c -> (g c)").partition_broadcast(P))
-        nc.scalar.dma_start(out=q_bf[:], in_=q.rearrange("g c -> (g c)").partition_broadcast(P))
+        p_bf = const.tile([P, GROUPS * P_COEFS], BF16)
+        q_bf = const.tile([P, GROUPS * Q_COEFS], BF16)
+        nc.scalar.dma_start(out=p_bf[:], in_=p.rearrange("g i -> (g i)").partition_broadcast(P))
+        nc.scalar.dma_start(out=q_bf[:], in_=q.rearrange("g i -> (g i)").partition_broadcast(P))
         one = const.tile([P, 1], F32)
         nc.vector.memset(one[:], 1.0)
 
         nc.vector.tensor_copy(out=b_rows[0 : GROUPS * OUT_TILES, :], in_=b_bf[:])
-        b_turned = psum.tile([P, HALF], F32, name="s_ps", bufs=3)
+        b_turned = psum.tile([P, HALF], F32, name="s_ps", bufs=psum_banks(AT_MULTIPLY, AT_QUAD))
         nc.tensor.transpose(b_turned[:, 0:P], b_rows[:], ident[:])
         b_cols = const.tile([P, GROUPS * OUT_TILES], F32)
         nc.vector.tensor_copy(out=b_cols[:], in_=b_turned[:, 0 : GROUPS * OUT_TILES])
-        p_f32 = const.tile([P, GROUPS * 4], F32)
-        q_f32 = const.tile([P, GROUPS * 3], F32)
+        p_f32 = const.tile([P, GROUPS * P_COEFS], F32)
+        q_f32 = const.tile([P, GROUPS * Q_COEFS], F32)
         nc.vector.tensor_copy(out=p_f32[:], in_=p_bf[:])
         nc.vector.tensor_copy(out=q_f32[:], in_=q_bf[:])
 
-        def due(step, at, count):
-            t = step - at
-            return t if 0 <= t < count else None
+        def run(stage, step, at, count):
+            if 0 <= step - at < count:
+                stage(step - at)
+
+        def quantise_if_complete(j):
+            if j % ROW_TILES == ROW_TILES - 1:
+                quantise_x(j // ROW_TILES)
 
         for step in range(AT_TURN_X, TILES + AT_FINISH):
-            j = due(step, AT_LOAD, PIECES)
-            if j is not None:
-                load_x(j)
+            run(load_x, step, AT_LOAD, PIECES)
 
-            j = due(step, AT_QUANTISE, PIECES)
-            t1, t2, t_out = due(step, AT_PRODUCT_1, TILES), due(step, AT_PRODUCT_2, TILES), due(step, AT_FINISH, TILES)
-            if j is not None and j % ROW_TILES == ROW_TILES - 1:
-                quantise_x(j // ROW_TILES)
-            if t2 is not None:
-                g = where(t2)[2]
-                plus_times_y(d3_sb, DEN, t2, "d3", 3, coef(q_f32, 3, g, 0))
-                plus_times_y(n3_sb, NUM, t2, "n3", 6, coef(p_f32, 4, g, 1))
-            if t1 is not None:
-                times_y(t1)
-            if t_out is not None:
-                finish(t_out)
+            run(quantise_if_complete, step, AT_QUANTISE, PIECES)
+            run(cubic, step, AT_CUBIC, TILES)
+            run(quadratic, step, AT_QUAD, TILES)
+            run(finish, step, AT_FINISH, TILES)
 
-            j, t = due(step, AT_GROUP_X, PIECES), due(step, AT_BIAS, TILES)
-            t_abs, t_root, t_square = due(step, AT_ABS, TILES), due(step, AT_ROOT, TILES), due(step, AT_SQUARE, TILES)
-            if j is not None:
-                group_x(j)
-            if t is not None:
-                add_bias(t)
-            if t_abs is not None:
-                absolute(t_abs)
-            if t_root is not None:
-                root_of_reciprocal(t_root)
-            if t_square is not None:
-                reciprocal(t_square)
+            run(group_x, step, AT_GROUP_X, PIECES)
+            run(add_bias, step, AT_BIAS, TILES)
+            run(absolute, step, AT_ABS, TILES)
+            run(root, step, AT_ROOT, TILES)
+            run(square, step, AT_SQUARE, TILES)
 
-            t = due(step, AT_LINEAR, TILES)
-            if t is not None:
-                linear(t)
+            run(linear, step, AT_LINEAR, TILES)
 
-            t_den, t_num = due(step, AT_TURN_DEN, TILES), due(step, AT_TURN_NUM, TILES)
-            j, t = due(step, AT_TURN_X, PIECES), due(step, AT_MULTIPLY, TILES)
-            if t_den is not None:
-                turn_back(den_ps, d3_sb, t_den, "den_ps")
-            if t_num is not None:
-                turn_back(num_ps, n3_sb, t_num, "num_ps")
-            if t is not None:
-                multiply(t)
-            if j is not None:
-                turn_x(j)
+            run(turn_den, step, AT_TURN_DEN, TILES)
+            run(turn_num, step, AT_TURN_NUM, TILES)
+            run(multiply, step, AT_MULTIPLY, TILES)
+            run(turn_x, step, AT_TURN_X, PIECES)

@@ -29,8 +29,9 @@ DEN, NUM = 0, 1
 P_COEFS, Q_COEFS = 4, 3
 
 AT_LOAD, AT_TURN_X, AT_GROUP_X, AT_QUANTISE = -15, -7, -6, -5
-AT_MULTIPLY, AT_BIAS, AT_LINEAR, AT_QUAD, AT_CUBIC, AT_TURN_DEN = -1, 0, 0, 1, 2, 3
+AT_MULTIPLY, AT_SQUARE_Y, AT_INNER, AT_PRODUCT, AT_OUTER_DEN, AT_OUTER_NUM, AT_TURN_DEN = -1, 0, 0, 1, 1, 2, 3
 AT_ABS, AT_ROOT, AT_SQUARE, AT_TURN_NUM, AT_FINISH = 4, 5, 6, 6, 7
+PAIR = 2
 
 PANEL_BUFS = 2
 STORE_BUFS = 3
@@ -55,7 +56,7 @@ def tile_groupkanlayer_e_kernel(tc, x, W_words, W_scales, b, p, q, out):
         ctx.enter_context(tc.manual_schedule())
 
         x_rows, x_turned, x_grouped, x_codes, x_scales = {}, {}, {}, {}, {}
-        s_ps, y_sb, lin_sb, quad_sb, den_sb, num_sb = {}, {}, {}, {}, {}, {}
+        s_ps, y2_sb, inner_sb, outer_sb, prod_sb = {}, {}, {}, {}, {}
         den_ps, num_ps, a_sb, u_sb, r_sb = {}, {}, {}, {}, {}
 
         def load_x(j):
@@ -96,7 +97,7 @@ def tile_groupkanlayer_e_kernel(tc, x, W_words, W_scales, b, p, q, out):
 
         def multiply(t):
             pan, ot, g = where(t)
-            s_ps[t] = psum.tile([P, HALF], F32, name="s_ps", bufs=psum_banks(AT_MULTIPLY, AT_QUAD))
+            s_ps[t] = psum.tile([P, HALF], F32, name="s_ps", bufs=psum_banks(AT_MULTIPLY, AT_PRODUCT))
             nc.tensor.matmul_mx(
                 out=s_ps[t][:],
                 lhsT=w_words[:, g, 2 * P * ot : 2 * P * (ot + 1)].bitcast(FP4X4),
@@ -107,60 +108,73 @@ def tile_groupkanlayer_e_kernel(tc, x, W_words, W_scales, b, p, q, out):
                 stop=True,
             )
 
-        def add_bias(t):
+        def square_y(t):
             pan, ot, g = where(t)
-            y_sb[t] = work.tile([P, HALF], F32, name="y", bufs=sbuf_slots(AT_BIAS, AT_CUBIC))
+            if t % PAIR == 0:
+                y2_sb[t // PAIR] = work.tile([P, PAIR, HALF], F32, name="y2", bufs=3)
             nc.scalar.activation(
-                out=y_sb[t][:], in_=s_ps[t][:], func=ACT.Identity,
+                out=y2_sb[t // PAIR][:, t % PAIR, :], in_=s_ps[t][:], func=ACT.Square,
                 bias=column(b_cols, OUT_TILES, g, ot), scale=1.0,
             )
 
-        def linear(t):
+        def inner(t):
             g = where(t)[2]
-            lin_sb[t] = work.tile([P, 2, HALF], F32, name="lin", bufs=sbuf_slots(AT_LINEAR, AT_QUAD))
+            inner_sb[t] = work.tile([P, 2, HALF], F32, name="inner", bufs=sbuf_slots(AT_INNER, AT_PRODUCT))
             nc.gpsimd.tensor_scalar(
-                out=lin_sb[t][:, DEN, :], in0=y_sb[t][:],
-                scalar1=column(q_f32, Q_COEFS, g, 2), scalar2=column(q_f32, Q_COEFS, g, 1),
+                out=inner_sb[t][:, DEN, :], in0=y2_sb[t // PAIR][:, t % PAIR, :],
+                scalar1=column(q_f32, Q_COEFS, g, 2), scalar2=column(q_f32, Q_COEFS, g, 0),
                 op0=ALU.mult, op1=ALU.add,
             )
             nc.gpsimd.tensor_scalar(
-                out=lin_sb[t][:, NUM, :], in0=y_sb[t][:],
-                scalar1=column(p_f32, P_COEFS, g, 3), scalar2=column(p_f32, P_COEFS, g, 2),
+                out=inner_sb[t][:, NUM, :], in0=y2_sb[t // PAIR][:, t % PAIR, :],
+                scalar1=column(p_f32, P_COEFS, g, 3), scalar2=column(p_f32, P_COEFS, g, 1),
                 op0=ALU.mult, op1=ALU.add,
             )
 
-        def quadratic(t):
+        def outer(t, plane, coef):
+            if t % PAIR != PAIR - 1:
+                return
+            j = t // PAIR
+            if plane == DEN:
+                outer_sb[j] = work.tile([P, 2, PAIR, HALF], F32, name="outer", bufs=5)
+            nc.gpsimd.tensor_scalar(
+                out=outer_sb[j][:, plane, :, :], in0=y2_sb[j][:],
+                scalar1=coef(where(t)[2]), scalar2=zero[:, 0:1], op0=ALU.mult, op1=ALU.add,
+            )
+
+        def outer_den(t):
+            outer(t, DEN, lambda g: column(q_f32, Q_COEFS, g, 1))
+
+        def outer_num(t):
+            outer(t, NUM, lambda g: column(p_f32, P_COEFS, g, 2))
+
+        def product(t):
             pan, ot, g = where(t)
-            quad_sb[t] = work.tile([P, 2, HALF], F32, name="quad", bufs=sbuf_slots(AT_QUAD, AT_CUBIC))
+            prod_sb[t] = work.tile([P, 2, HALF], F32, name="prod", bufs=sbuf_slots(AT_PRODUCT, AT_TURN_NUM))
             nc.vector.scalar_tensor_tensor(
-                out=quad_sb[t][:], in0=s_ps[t][:].unsqueeze(1).to_broadcast([P, 2, HALF]),
-                scalar=column(b_cols, OUT_TILES, g, ot), in1=lin_sb[t][:], op0=ALU.add, op1=ALU.mult,
+                out=prod_sb[t][:], in0=s_ps[t][:].unsqueeze(1).to_broadcast([P, 2, HALF]),
+                scalar=column(b_cols, OUT_TILES, g, ot), in1=inner_sb[t][:], op0=ALU.add, op1=ALU.mult,
             )
 
-        def cubic(t):
-            g = where(t)[2]
-            den_sb[t] = work.tile([P, HALF], F32, name="den", bufs=sbuf_slots(AT_CUBIC, AT_TURN_DEN))
-            nc.vector.scalar_tensor_tensor(
-                out=den_sb[t][:], in0=quad_sb[t][:, DEN, :], scalar=column(q_f32, Q_COEFS, g, 0),
-                in1=y_sb[t][:], op0=ALU.add, op1=ALU.mult,
-            )
-            num_sb[t] = work.tile([P, HALF], F32, name="num", bufs=sbuf_slots(AT_CUBIC, AT_TURN_NUM))
-            nc.vector.scalar_tensor_tensor(
-                out=num_sb[t][:], in0=quad_sb[t][:, NUM, :], scalar=column(p_f32, P_COEFS, g, 1),
-                in1=y_sb[t][:], op0=ALU.add, op1=ALU.mult,
-            )
-
-        def turn_back(turned, src):
+        def turn_back(turned, t, plane):
             for rt in range(ROW_TILES):
-                nc.tensor.transpose(turned[:, rt, :], src[:, rt * P : (rt + 1) * P], ident[:])
+                cols = slice(rt * P, (rt + 1) * P)
+                nc.tensor.matmul(
+                    out=turned[:, rt, :], lhsT=outer_sb[t // PAIR][:, plane, t % PAIR, cols], rhs=ident[:],
+                    is_transpose=True, start=True, stop=False,
+                )
+                nc.tensor.matmul(
+                    out=turned[:, rt, :], lhsT=prod_sb[t][:, plane, cols], rhs=ident[:],
+                    is_transpose=True, start=False, stop=True,
+                )
 
         def turn_den(t):
             den_ps[t] = psum.tile([P, ROW_TILES, P], F32, name="den_ps", bufs=psum_banks(AT_TURN_DEN, AT_ABS))
-            turn_back(den_ps[t], den_sb[t])
+            turn_back(den_ps[t], t, DEN)
 
         def turn_num(t):
             num_ps[t] = psum.tile([P, ROW_TILES, P], F32, name="num_ps", bufs=psum_banks(AT_TURN_NUM, AT_FINISH))
-            turn_back(num_ps[t], num_sb[t])
+            turn_back(num_ps[t], t, NUM)
 
         def absolute(t):
             a_sb[t] = work.tile([P, ROW_TILES, P], F32, name="a", bufs=sbuf_slots(AT_ABS, AT_ROOT))
@@ -218,9 +232,11 @@ def tile_groupkanlayer_e_kernel(tc, x, W_words, W_scales, b, p, q, out):
         nc.scalar.dma_start(out=q_bf[:], in_=q.rearrange("g i -> (g i)").partition_broadcast(P))
         one = const.tile([P, 1], F32)
         nc.vector.memset(one[:], 1.0)
+        zero = const.tile([P, 1], F32)
+        nc.vector.memset(zero[:], 0.0)
 
         nc.vector.tensor_copy(out=b_rows[0 : GROUPS * OUT_TILES, :], in_=b_bf[:])
-        b_turned = psum.tile([P, HALF], F32, name="s_ps", bufs=psum_banks(AT_MULTIPLY, AT_QUAD))
+        b_turned = psum.tile([P, HALF], F32, name="s_ps", bufs=psum_banks(AT_MULTIPLY, AT_PRODUCT))
         nc.tensor.transpose(b_turned[:, 0:P], b_rows[:], ident[:])
         b_cols = const.tile([P, GROUPS * OUT_TILES], F32)
         nc.vector.tensor_copy(out=b_cols[:], in_=b_turned[:, 0 : GROUPS * OUT_TILES])
@@ -241,17 +257,18 @@ def tile_groupkanlayer_e_kernel(tc, x, W_words, W_scales, b, p, q, out):
             run(load_x, step, AT_LOAD, PIECES)
 
             run(quantise_if_complete, step, AT_QUANTISE, PIECES)
-            run(cubic, step, AT_CUBIC, TILES)
-            run(quadratic, step, AT_QUAD, TILES)
             run(finish, step, AT_FINISH, TILES)
+            run(product, step, AT_PRODUCT, TILES)
 
             run(group_x, step, AT_GROUP_X, PIECES)
-            run(add_bias, step, AT_BIAS, TILES)
+            run(square_y, step, AT_SQUARE_Y, TILES)
             run(absolute, step, AT_ABS, TILES)
             run(root, step, AT_ROOT, TILES)
             run(square, step, AT_SQUARE, TILES)
 
-            run(linear, step, AT_LINEAR, TILES)
+            run(outer_den, step, AT_OUTER_DEN, TILES)
+            run(outer_num, step, AT_OUTER_NUM, TILES)
+            run(inner, step, AT_INNER, TILES)
 
             run(turn_den, step, AT_TURN_DEN, TILES)
             run(turn_num, step, AT_TURN_NUM, TILES)

@@ -29,8 +29,8 @@ DEN, NUM = 0, 1
 P_COEFS, Q_COEFS = 4, 3
 
 AT_LOAD, AT_TURN_X, AT_GROUP_X, AT_QUANTISE = -15, -7, -6, -5
-AT_MULTIPLY, AT_SQUARE_Y, AT_INNER, AT_PRODUCT, AT_OUTER_DEN, AT_OUTER_NUM, AT_TURN_DEN = -1, 0, 0, 1, 1, 2, 3
-AT_ABS, AT_ROOT, AT_SQUARE, AT_TURN_NUM, AT_FINISH = 4, 5, 6, 6, 7
+AT_MULTIPLY, AT_SQUARE_Y, AT_INNER, AT_INNER_DEN, AT_PRODUCT, AT_OUTER_NUM, AT_TURN_DEN = -1, 0, 0, 1, 1, 1, 2
+AT_ABS, AT_ROOT, AT_SQUARE, AT_TURN_NUM, AT_FINISH = 3, 4, 5, 5, 6
 PAIR = 2
 
 PANEL_BUFS = 2
@@ -56,7 +56,7 @@ def tile_groupkanlayer_e_kernel(tc, x, W_words, W_scales, b, p, q, out):
         ctx.enter_context(tc.manual_schedule())
 
         x_rows, x_turned, x_grouped, x_codes, x_scales = {}, {}, {}, {}, {}
-        s_ps, y2_sb, inner_sb, outer_sb, prod_sb = {}, {}, {}, {}, {}
+        s_ps, y2_sb, part_sb, inner_sb, outer_sb, prod_sb = {}, {}, {}, {}, {}, {}
         den_ps, num_ps, a_sb, u_sb, r_sb = {}, {}, {}, {}, {}
 
         def load_x(j):
@@ -97,7 +97,8 @@ def tile_groupkanlayer_e_kernel(tc, x, W_words, W_scales, b, p, q, out):
 
         def multiply(t):
             pan, ot, g = where(t)
-            s_ps[t] = psum.tile([P, HALF], F32, name="s_ps", bufs=psum_banks(AT_MULTIPLY, AT_PRODUCT))
+            if t not in s_ps:
+                s_ps[t] = psum.tile([P, HALF], F32, name="s_ps", bufs=psum_banks(AT_MULTIPLY, AT_PRODUCT))
             nc.tensor.matmul_mx(
                 out=s_ps[t][:],
                 lhsT=w_words[:, g, 2 * P * ot : 2 * P * (ot + 1)].bitcast(FP4X4),
@@ -118,35 +119,36 @@ def tile_groupkanlayer_e_kernel(tc, x, W_words, W_scales, b, p, q, out):
             )
 
         def inner(t):
-            g = where(t)[2]
-            inner_sb[t] = work.tile([P, 2, HALF], F32, name="inner", bufs=sbuf_slots(AT_INNER, AT_PRODUCT))
+            pan, ot, g = where(t)
+            part_sb[t] = work.tile([P, HALF], F32, name="part", bufs=sbuf_slots(AT_INNER, AT_INNER_DEN))
             nc.gpsimd.tensor_scalar(
-                out=inner_sb[t][:, DEN, :], in0=y2_sb[t // PAIR][:, t % PAIR, :],
-                scalar1=column(q_f32, Q_COEFS, g, 2), scalar2=column(q_f32, Q_COEFS, g, 0),
+                out=part_sb[t][:], in0=y2_sb[t // PAIR][:, t % PAIR, :],
+                scalar1=column(q_f32, Q_COEFS, g, 2), scalar2=column(k_cols, OUT_TILES, g, ot),
                 op0=ALU.mult, op1=ALU.add,
             )
+            inner_sb[t] = work.tile([P, 2, HALF], F32, name="inner", bufs=sbuf_slots(AT_INNER, AT_PRODUCT))
             nc.gpsimd.tensor_scalar(
                 out=inner_sb[t][:, NUM, :], in0=y2_sb[t // PAIR][:, t % PAIR, :],
                 scalar1=column(p_f32, P_COEFS, g, 3), scalar2=column(p_f32, P_COEFS, g, 1),
                 op0=ALU.mult, op1=ALU.add,
             )
 
-        def outer(t, plane, coef):
+        def inner_den(t):
+            g = where(t)[2]
+            nc.vector.scalar_tensor_tensor(
+                out=inner_sb[t][:, DEN, :], in0=s_ps[t][:], scalar=column(q_f32, Q_COEFS, g, 1),
+                in1=part_sb[t][:], op0=ALU.mult, op1=ALU.add,
+            )
+
+        def outer_num(t):
             if t % PAIR != PAIR - 1:
                 return
             j = t // PAIR
-            if plane == DEN:
-                outer_sb[j] = work.tile([P, 2, PAIR, HALF], F32, name="outer", bufs=5)
+            outer_sb[j] = work.tile([P, PAIR, HALF], F32, name="outer", bufs=5)
             nc.gpsimd.tensor_scalar(
-                out=outer_sb[j][:, plane, :, :], in0=y2_sb[j][:],
-                scalar1=coef(where(t)[2]), scalar2=zero[:, 0:1], op0=ALU.mult, op1=ALU.add,
+                out=outer_sb[j][:], in0=y2_sb[j][:],
+                scalar1=column(p_f32, P_COEFS, where(t)[2], 2), scalar2=zero[:, 0:1], op0=ALU.mult, op1=ALU.add,
             )
-
-        def outer_den(t):
-            outer(t, DEN, lambda g: column(q_f32, Q_COEFS, g, 1))
-
-        def outer_num(t):
-            outer(t, NUM, lambda g: column(p_f32, P_COEFS, g, 2))
 
         def product(t):
             pan, ot, g = where(t)
@@ -156,25 +158,23 @@ def tile_groupkanlayer_e_kernel(tc, x, W_words, W_scales, b, p, q, out):
                 scalar=column(b_cols, OUT_TILES, g, ot), in1=inner_sb[t][:], op0=ALU.add, op1=ALU.mult,
             )
 
-        def turn_back(turned, t, plane):
-            for rt in range(ROW_TILES):
-                cols = slice(rt * P, (rt + 1) * P)
-                nc.tensor.matmul(
-                    out=turned[:, rt, :], lhsT=outer_sb[t // PAIR][:, plane, t % PAIR, cols], rhs=ident[:],
-                    is_transpose=True, start=True, stop=False,
-                )
-                nc.tensor.matmul(
-                    out=turned[:, rt, :], lhsT=prod_sb[t][:, plane, cols], rhs=ident[:],
-                    is_transpose=True, start=False, stop=True,
-                )
-
         def turn_den(t):
             den_ps[t] = psum.tile([P, ROW_TILES, P], F32, name="den_ps", bufs=psum_banks(AT_TURN_DEN, AT_ABS))
-            turn_back(den_ps[t], t, DEN)
+            for rt in range(ROW_TILES):
+                nc.tensor.transpose(den_ps[t][:, rt, :], prod_sb[t][:, DEN, rt * P : (rt + 1) * P], ident[:])
 
         def turn_num(t):
             num_ps[t] = psum.tile([P, ROW_TILES, P], F32, name="num_ps", bufs=psum_banks(AT_TURN_NUM, AT_FINISH))
-            turn_back(num_ps[t], t, NUM)
+            for rt in range(ROW_TILES):
+                cols = slice(rt * P, (rt + 1) * P)
+                nc.tensor.matmul(
+                    out=num_ps[t][:, rt, :], lhsT=outer_sb[t // PAIR][:, t % PAIR, cols], rhs=ident[:],
+                    is_transpose=True, start=True, stop=False,
+                )
+                nc.tensor.matmul(
+                    out=num_ps[t][:, rt, :], lhsT=prod_sb[t][:, NUM, cols], rhs=ident[:],
+                    is_transpose=True, start=False, stop=True,
+                )
 
         def absolute(t):
             a_sb[t] = work.tile([P, ROW_TILES, P], F32, name="a", bufs=sbuf_slots(AT_ABS, AT_ROOT))
@@ -244,6 +244,13 @@ def tile_groupkanlayer_e_kernel(tc, x, W_words, W_scales, b, p, q, out):
         q_f32 = const.tile([P, GROUPS * Q_COEFS], F32)
         nc.vector.tensor_copy(out=p_f32[:], in_=p_bf[:])
         nc.vector.tensor_copy(out=q_f32[:], in_=q_bf[:])
+        k_cols = const.tile([P, GROUPS * OUT_TILES], F32)
+        for g in range(GROUPS):
+            nc.vector.tensor_scalar(
+                out=k_cols[:, OUT_TILES * g : OUT_TILES * (g + 1)], in0=b_cols[:, OUT_TILES * g : OUT_TILES * (g + 1)],
+                scalar1=column(q_f32, Q_COEFS, g, 1), scalar2=column(q_f32, Q_COEFS, g, 0),
+                op0=ALU.mult, op1=ALU.add,
+            )
 
         def run(stage, step, at, count):
             if 0 <= step - at < count:
@@ -256,9 +263,10 @@ def tile_groupkanlayer_e_kernel(tc, x, W_words, W_scales, b, p, q, out):
         for step in range(AT_TURN_X, TILES + AT_FINISH):
             run(load_x, step, AT_LOAD, PIECES)
 
-            run(quantise_if_complete, step, AT_QUANTISE, PIECES)
+            run(inner_den, step, AT_INNER_DEN, TILES)
             run(finish, step, AT_FINISH, TILES)
             run(product, step, AT_PRODUCT, TILES)
+            run(quantise_if_complete, step, AT_QUANTISE, PIECES)
 
             run(group_x, step, AT_GROUP_X, PIECES)
             run(square_y, step, AT_SQUARE_Y, TILES)
@@ -266,11 +274,11 @@ def tile_groupkanlayer_e_kernel(tc, x, W_words, W_scales, b, p, q, out):
             run(root, step, AT_ROOT, TILES)
             run(square, step, AT_SQUARE, TILES)
 
-            run(outer_den, step, AT_OUTER_DEN, TILES)
             run(outer_num, step, AT_OUTER_NUM, TILES)
             run(inner, step, AT_INNER, TILES)
 
             run(turn_den, step, AT_TURN_DEN, TILES)
+            run(multiply, step, AT_MULTIPLY, TILES)
             run(turn_num, step, AT_TURN_NUM, TILES)
             run(multiply, step, AT_MULTIPLY, TILES)
             run(turn_x, step, AT_TURN_X, PIECES)

@@ -278,7 +278,6 @@ def tile_groupkanlayer_e_kernel(tc, x, W_words, W_scales, b, p, q, out):
             run(inner, step, AT_INNER, TILES)
 
             run(turn_den, step, AT_TURN_DEN, TILES)
-            run(multiply, step, AT_MULTIPLY, TILES)
             run(turn_num, step, AT_TURN_NUM, TILES)
             run(multiply, step, AT_MULTIPLY, TILES)
             run(turn_x, step, AT_TURN_X, PIECES)

@@ -160,12 +160,14 @@ def tile_groupkanlayer_e_kernel(tc, x, W_words, W_scales, b, p, q, out):
 
         def turn_den(t):
             den_ps[t] = psum.tile([P, ROW_TILES, P], F32, name="den_ps", bufs=psum_banks(AT_TURN_DEN, AT_ABS))
-            for rt in range(ROW_TILES):
+            nc.tensor.matmul(out=den_ps[t][:, 0, :], lhsT=prod_sb[t][:, DEN, 0:P], rhs=ident[:], start=True, stop=True)
+            for rt in range(1, ROW_TILES):
                 nc.tensor.transpose(den_ps[t][:, rt, :], prod_sb[t][:, DEN, rt * P : (rt + 1) * P], ident[:])
 
-        def turn_num(t):
-            num_ps[t] = psum.tile([P, ROW_TILES, P], F32, name="num_ps", bufs=psum_banks(AT_TURN_NUM, AT_FINISH))
-            for rt in range(ROW_TILES):
+        def turn_num(t, row_tiles):
+            if t not in num_ps:
+                num_ps[t] = psum.tile([P, ROW_TILES, P], F32, name="num_ps", bufs=psum_banks(AT_TURN_NUM, AT_FINISH))
+            for rt in row_tiles:
                 cols = slice(rt * P, (rt + 1) * P)
                 nc.tensor.matmul(
                     out=num_ps[t][:, rt, :], lhsT=outer_sb[t // PAIR][:, t % PAIR, cols], rhs=ident[:],
@@ -278,6 +280,8 @@ def tile_groupkanlayer_e_kernel(tc, x, W_words, W_scales, b, p, q, out):
             run(inner, step, AT_INNER, TILES)
 
             run(turn_den, step, AT_TURN_DEN, TILES)
-            run(turn_num, step, AT_TURN_NUM, TILES)
+            run(lambda t: turn_num(t, range(0, ROW_TILES // 2)), step, AT_TURN_NUM, TILES)
             run(multiply, step, AT_MULTIPLY, TILES)
+            run(multiply, step, AT_MULTIPLY, TILES)
+            run(lambda t: turn_num(t, range(ROW_TILES // 2, ROW_TILES)), step, AT_TURN_NUM, TILES)
             run(turn_x, step, AT_TURN_X, PIECES)

@@ -32,6 +32,7 @@ AT_LOAD, AT_TURN_X, AT_GROUP_X, AT_QUANTISE = -15, -7, -6, -5
 AT_MULTIPLY, AT_SQUARE_Y, AT_INNER, AT_INNER_DEN, AT_PRODUCT, AT_OUTER_NUM, AT_TURN_DEN = -1, 0, 0, 1, 1, 1, 2
 AT_ABS, AT_ROOT, AT_SQUARE, AT_TURN_NUM, AT_FINISH = 3, 4, 5, 5, 6
 PAIR = 2
+SCALED_BY_MATMUL = 1
 
 PANEL_BUFS = 2
 STORE_BUFS = 3
@@ -68,7 +69,12 @@ def tile_groupkanlayer_e_kernel(tc, x, W_words, W_scales, b, p, q, out):
 
         def turn_x(j):
             words = x_rows[j][:].bitcast(F32)
-            x_turned[j] = psum.tile([P, 2, P], F32, name="x_turned", bufs=1)
+            if j < ROW_TILES // 2:
+                x_turned[j] = psum.tile([P, 2, P], F32, name="den_ps", bufs=psum_banks(AT_TURN_DEN, AT_ABS))
+            elif j < ROW_TILES:
+                x_turned[j] = psum.tile([P, 2, P], F32, name="num_ps", bufs=psum_banks(AT_TURN_NUM, AT_FINISH))
+            else:
+                x_turned[j] = psum.tile([P, 2, P], F32, name="x_turned", bufs=1)
             for w in range(2):
                 nc.tensor.transpose(x_turned[j][:, w, :], words[:, w : GIN // 2 : 2], ident[:])
 
@@ -112,7 +118,7 @@ def tile_groupkanlayer_e_kernel(tc, x, W_words, W_scales, b, p, q, out):
         def square_y(t):
             pan, ot, g = where(t)
             if t % PAIR == 0:
-                y2_sb[t // PAIR] = work.tile([P, PAIR, HALF], F32, name="y2", bufs=3)
+                y2_sb[t // PAIR] = work.tile([P, PAIR, HALF], F32, name="y2", bufs=5)
             nc.scalar.activation(
                 out=y2_sb[t // PAIR][:, t % PAIR, :], in_=s_ps[t][:], func=ACT.Square,
                 bias=column(b_cols, OUT_TILES, g, ot), scale=1.0,
@@ -145,8 +151,9 @@ def tile_groupkanlayer_e_kernel(tc, x, W_words, W_scales, b, p, q, out):
                 return
             j = t // PAIR
             outer_sb[j] = work.tile([P, PAIR, HALF], F32, name="outer", bufs=5)
+            rest = slice(SCALED_BY_MATMUL * P, HALF)
             nc.gpsimd.tensor_scalar(
-                out=outer_sb[j][:], in0=y2_sb[j][:],
+                out=outer_sb[j][:, :, rest], in0=y2_sb[j][:, :, rest],
                 scalar1=column(p_f32, P_COEFS, where(t)[2], 2), scalar2=zero[:, 0:1], op0=ALU.mult, op1=ALU.add,
             )
 
@@ -160,8 +167,7 @@ def tile_groupkanlayer_e_kernel(tc, x, W_words, W_scales, b, p, q, out):
 
         def turn_den(t):
             den_ps[t] = psum.tile([P, ROW_TILES, P], F32, name="den_ps", bufs=psum_banks(AT_TURN_DEN, AT_ABS))
-            nc.tensor.matmul(out=den_ps[t][:, 0, :], lhsT=prod_sb[t][:, DEN, 0:P], rhs=ident[:], start=True, stop=True)
-            for rt in range(1, ROW_TILES):
+            for rt in range(ROW_TILES):
                 nc.tensor.transpose(den_ps[t][:, rt, :], prod_sb[t][:, DEN, rt * P : (rt + 1) * P], ident[:])
 
         def turn_num(t, row_tiles):
@@ -169,10 +175,16 @@ def tile_groupkanlayer_e_kernel(tc, x, W_words, W_scales, b, p, q, out):
                 num_ps[t] = psum.tile([P, ROW_TILES, P], F32, name="num_ps", bufs=psum_banks(AT_TURN_NUM, AT_FINISH))
             for rt in row_tiles:
                 cols = slice(rt * P, (rt + 1) * P)
-                nc.tensor.matmul(
-                    out=num_ps[t][:, rt, :], lhsT=outer_sb[t // PAIR][:, t % PAIR, cols], rhs=ident[:],
-                    is_transpose=True, start=True, stop=False,
-                )
+                if rt < SCALED_BY_MATMUL:
+                    nc.tensor.matmul(
+                        out=num_ps[t][:, rt, :], lhsT=y2_sb[t // PAIR][:, t % PAIR, cols],
+                        rhs=p2_diag[:, where(t)[2], :], start=True, stop=False,
+                    )
+                else:
+                    nc.tensor.matmul(
+                        out=num_ps[t][:, rt, :], lhsT=outer_sb[t // PAIR][:, t % PAIR, cols], rhs=ident[:],
+                        is_transpose=True, start=True, stop=False,
+                    )
                 nc.tensor.matmul(
                     out=num_ps[t][:, rt, :], lhsT=prod_sb[t][:, NUM, cols], rhs=ident[:],
                     is_transpose=True, start=False, stop=True,
@@ -246,6 +258,11 @@ def tile_groupkanlayer_e_kernel(tc, x, W_words, W_scales, b, p, q, out):
         q_f32 = const.tile([P, GROUPS * Q_COEFS], F32)
         nc.vector.tensor_copy(out=p_f32[:], in_=p_bf[:])
         nc.vector.tensor_copy(out=q_f32[:], in_=q_bf[:])
+        p2_diag = const.tile([P, GROUPS, P], F32)
+        for g in range(GROUPS):
+            nc.vector.tensor_scalar(
+                out=p2_diag[:, g, :], in0=ident[:], scalar1=column(p_f32, P_COEFS, g, 2), scalar2=None, op0=ALU.mult,
+            )
         k_cols = const.tile([P, GROUPS * OUT_TILES], F32)
         for g in range(GROUPS):
             nc.vector.tensor_scalar(
@@ -279,8 +296,8 @@ def tile_groupkanlayer_e_kernel(tc, x, W_words, W_scales, b, p, q, out):
             run(outer_num, step, AT_OUTER_NUM, TILES)
             run(inner, step, AT_INNER, TILES)
 
-            run(turn_den, step, AT_TURN_DEN, TILES)
             run(lambda t: turn_num(t, range(0, ROW_TILES // 2)), step, AT_TURN_NUM, TILES)
+            run(turn_den, step, AT_TURN_DEN, TILES)
             run(multiply, step, AT_MULTIPLY, TILES)
             run(multiply, step, AT_MULTIPLY, TILES)
             run(lambda t: turn_num(t, range(ROW_TILES // 2, ROW_TILES)), step, AT_TURN_NUM, TILES)

@@ -32,7 +32,7 @@ AT_LOAD, AT_TURN_X, AT_GROUP_X, AT_QUANTISE = -15, -7, -6, -5
 AT_MULTIPLY, AT_SQUARE_Y, AT_INNER, AT_INNER_DEN, AT_PRODUCT, AT_OUTER_NUM, AT_TURN_DEN = -1, 0, 0, 1, 1, 1, 2
 AT_ABS, AT_ROOT, AT_SQUARE, AT_TURN_NUM, AT_FINISH = 3, 4, 5, 5, 6
 PAIR = 2
-SCALED_BY_MATMUL = 1
+
 
 PANEL_BUFS = 2
 STORE_BUFS = 3
@@ -73,19 +73,25 @@ def tile_groupkanlayer_e_kernel(tc, x, W_words, W_scales, b, p, q, out):
                 x_turned[j] = psum.tile([P, 2, P], F32, name="den_ps", bufs=psum_banks(AT_TURN_DEN, AT_ABS))
             elif j < ROW_TILES:
                 x_turned[j] = psum.tile([P, 2, P], F32, name="num_ps", bufs=psum_banks(AT_TURN_NUM, AT_FINISH))
+            elif j == ROW_TILES:
+                x_turned[j] = psum.tile([P, 2, P], F32, name="s_ps", bufs=psum_banks(AT_MULTIPLY, AT_PRODUCT))
             else:
                 x_turned[j] = psum.tile([P, 2, P], F32, name="x_turned", bufs=1)
             for w in range(2):
                 nc.tensor.transpose(x_turned[j][:, w, :], words[:, w : GIN // 2 : 2], ident[:])
 
-        def group_x(j):
+        def group_x(j, by_vector):
+            if by_vector != (j < ROW_TILES and j % 2 == 1):
+                return
             pan, rt = divmod(j, ROW_TILES)
             if rt == 0:
                 x_grouped[pan] = work.tile([P, 4 * HALF], BF16, name="x_grouped", bufs=PANEL_BUFS, align_bytes=64)
-            nc.scalar.copy(
-                out=x_grouped[pan][:, 4 * P * rt : 4 * P * (rt + 1)].bitcast(F32).rearrange("pp (n w) -> pp n w", w=2),
-                in_=x_turned[j][:].rearrange("pp w n -> pp n w"),
-            )
+            dst = x_grouped[pan][:, 4 * P * rt : 4 * P * (rt + 1)].bitcast(F32).rearrange("pp (n w) -> pp n w", w=2)
+            src = x_turned[j][:].rearrange("pp w n -> pp n w")
+            if by_vector:
+                nc.vector.tensor_copy(out=dst, in_=src)
+            else:
+                nc.scalar.copy(out=dst, in_=src)
 
         def quantise_x(pan):
             x_codes[pan] = work.tile([P, HALF], U32, name="x_codes", bufs=PANEL_BUFS, align_bytes=64)
@@ -100,6 +106,9 @@ def tile_groupkanlayer_e_kernel(tc, x, W_words, W_scales, b, p, q, out):
 
         def column(table, width, g, i):
             return table[:, width * g + i : width * g + i + 1]
+
+        def blocks_by_matmul(j):
+            return (0, ROW_TILES - 1) if j % 2 == 1 else (0,)
 
         def multiply(t):
             pan, ot, g = where(t)
@@ -151,7 +160,7 @@ def tile_groupkanlayer_e_kernel(tc, x, W_words, W_scales, b, p, q, out):
                 return
             j = t // PAIR
             outer_sb[j] = work.tile([P, PAIR, HALF], F32, name="outer", bufs=5)
-            rest = slice(SCALED_BY_MATMUL * P, HALF)
+            rest = slice(P, HALF - (len(blocks_by_matmul(j)) - 1) * P)
             nc.gpsimd.tensor_scalar(
                 out=outer_sb[j][:, :, rest], in0=y2_sb[j][:, :, rest],
                 scalar1=column(p_f32, P_COEFS, where(t)[2], 2), scalar2=zero[:, 0:1], op0=ALU.mult, op1=ALU.add,
@@ -175,7 +184,7 @@ def tile_groupkanlayer_e_kernel(tc, x, W_words, W_scales, b, p, q, out):
                 num_ps[t] = psum.tile([P, ROW_TILES, P], F32, name="num_ps", bufs=psum_banks(AT_TURN_NUM, AT_FINISH))
             for rt in row_tiles:
                 cols = slice(rt * P, (rt + 1) * P)
-                if rt < SCALED_BY_MATMUL:
+                if rt in blocks_by_matmul(t // PAIR):
                     nc.tensor.matmul(
                         out=num_ps[t][:, rt, :], lhsT=y2_sb[t // PAIR][:, t % PAIR, cols],
                         rhs=p2_diag[:, where(t)[2], :], start=True, stop=False,
@@ -285,10 +294,11 @@ def tile_groupkanlayer_e_kernel(tc, x, W_words, W_scales, b, p, q, out):
             run(inner_den, step, AT_INNER_DEN, TILES)
             run(finish, step, AT_FINISH, TILES)
             run(product, step, AT_PRODUCT, TILES)
+            run(lambda j: group_x(j, True), step, AT_GROUP_X, PIECES)
             run(quantise_if_complete, step, AT_QUANTISE, PIECES)
 
-            run(group_x, step, AT_GROUP_X, PIECES)
             run(square_y, step, AT_SQUARE_Y, TILES)
+            run(lambda j: group_x(j, False), step, AT_GROUP_X, PIECES)
             run(absolute, step, AT_ABS, TILES)
             run(root, step, AT_ROOT, TILES)
             run(square, step, AT_SQUARE, TILES)

@@ -309,6 +309,5 @@ def tile_groupkanlayer_e_kernel(tc, x, W_words, W_scales, b, p, q, out):
             run(lambda t: turn_num(t, range(0, ROW_TILES // 2)), step, AT_TURN_NUM, TILES)
             run(turn_den, step, AT_TURN_DEN, TILES)
             run(multiply, step, AT_MULTIPLY, TILES)
-            run(multiply, step, AT_MULTIPLY, TILES)
             run(lambda t: turn_num(t, range(ROW_TILES // 2, ROW_TILES)), step, AT_TURN_NUM, TILES)
             run(turn_x, step, AT_TURN_X, PIECES)

@@ -25,14 +25,13 @@ OUT_TILES = GOUT // P
 PANELS = GROUPS * HALVES
 TILES = PANELS * OUT_TILES
 PIECES = PANELS * ROW_TILES
-DEN, NUM = 0, 1
+NUM, DEN = 0, 1
 P_COEFS, Q_COEFS = 4, 3
 
 AT_LOAD, AT_TURN_X, AT_GROUP_X, AT_QUANTISE = -15, -7, -6, -5
-AT_MULTIPLY, AT_SQUARE_Y, AT_INNER, AT_INNER_DEN, AT_PRODUCT, AT_OUTER_NUM, AT_TURN_DEN = -1, 0, 0, 1, 1, 1, 2
+AT_MULTIPLY, AT_SQUARE_Y, AT_PRODUCT, AT_AFFINE, AT_TURN_DEN = -1, 0, 1, 1, 2
 AT_ABS, AT_ROOT, AT_SQUARE, AT_TURN_NUM, AT_FINISH = 3, 4, 5, 5, 6
-PAIR = 2
-
+TINY = 2.0**-60
 
 PANEL_BUFS = 2
 STORE_BUFS = 3
@@ -57,7 +56,7 @@ def tile_groupkanlayer_e_kernel(tc, x, W_words, W_scales, b, p, q, out):
         ctx.enter_context(tc.manual_schedule())
 
         x_rows, x_turned, x_grouped, x_codes, x_scales = {}, {}, {}, {}, {}
-        s_ps, y2_sb, part_sb, inner_sb, outer_sb, prod_sb = {}, {}, {}, {}, {}, {}
+        s_ps, y2_sb, affine_sb, prod_sb = {}, {}, {}, {}
         den_ps, num_ps, a_sb, u_sb, r_sb = {}, {}, {}, {}, {}
 
         def load_x(j):
@@ -81,7 +80,7 @@ def tile_groupkanlayer_e_kernel(tc, x, W_words, W_scales, b, p, q, out):
                 nc.tensor.transpose(x_turned[j][:, w, :], words[:, w : GIN // 2 : 2], ident[:])
 
         def group_x(j, by_vector):
-            if by_vector != (j < ROW_TILES and j % 2 == 1):
+            if by_vector == (j < ROW_TILES and j % 2 == 0):
                 return
             pan, rt = divmod(j, ROW_TILES)
             if rt == 0:
@@ -107,9 +106,6 @@ def tile_groupkanlayer_e_kernel(tc, x, W_words, W_scales, b, p, q, out):
         def column(table, width, g, i):
             return table[:, width * g + i : width * g + i + 1]
 
-        def blocks_by_matmul(j):
-            return (0, ROW_TILES - 1) if j % 2 == 1 else (0,)
-
         def multiply(t):
             pan, ot, g = where(t)
             if t not in s_ps:
@@ -126,82 +122,60 @@ def tile_groupkanlayer_e_kernel(tc, x, W_words, W_scales, b, p, q, out):
 
         def square_y(t):
             pan, ot, g = where(t)
-            if t % PAIR == 0:
-                y2_sb[t // PAIR] = work.tile([P, PAIR, HALF], F32, name="y2", bufs=5)
+            y2_sb[t] = work.tile([P, HALF], F32, name="y2", bufs=sbuf_slots(AT_SQUARE_Y, AT_PRODUCT))
             nc.scalar.activation(
-                out=y2_sb[t // PAIR][:, t % PAIR, :], in_=s_ps[t][:], func=ACT.Square,
-                bias=column(b_cols, OUT_TILES, g, ot), scale=1.0,
+                out=y2_sb[t][:], in_=s_ps[t][:], func=ACT.Square, bias=column(b_cols, OUT_TILES, g, ot), scale=1.0,
             )
 
-        def inner(t):
+        def affine(t):
             pan, ot, g = where(t)
-            part_sb[t] = work.tile([P, HALF], F32, name="part", bufs=sbuf_slots(AT_INNER, AT_INNER_DEN))
-            nc.gpsimd.tensor_scalar(
-                out=part_sb[t][:], in0=y2_sb[t // PAIR][:, t % PAIR, :],
-                scalar1=column(q_f32, Q_COEFS, g, 2), scalar2=column(k_cols, OUT_TILES, g, ot),
-                op0=ALU.mult, op1=ALU.add,
-            )
-            inner_sb[t] = work.tile([P, 2, HALF], F32, name="inner", bufs=sbuf_slots(AT_INNER, AT_PRODUCT))
-            nc.gpsimd.tensor_scalar(
-                out=inner_sb[t][:, NUM, :], in0=y2_sb[t // PAIR][:, t % PAIR, :],
-                scalar1=column(p_f32, P_COEFS, g, 3), scalar2=column(p_f32, P_COEFS, g, 1),
-                op0=ALU.mult, op1=ALU.add,
-            )
-
-        def inner_den(t):
-            g = where(t)[2]
-            nc.vector.scalar_tensor_tensor(
-                out=inner_sb[t][:, DEN, :], in0=s_ps[t][:], scalar=column(q_f32, Q_COEFS, g, 1),
-                in1=part_sb[t][:], op0=ALU.mult, op1=ALU.add,
-            )
-
-        def outer_num(t):
-            if t % PAIR != PAIR - 1:
-                return
-            j = t // PAIR
-            outer_sb[j] = work.tile([P, PAIR, HALF], F32, name="outer", bufs=5)
-            rest = slice(P, HALF - (len(blocks_by_matmul(j)) - 1) * P)
-            nc.gpsimd.tensor_scalar(
-                out=outer_sb[j][:, :, rest], in0=y2_sb[j][:, :, rest],
-                scalar1=column(p_f32, P_COEFS, where(t)[2], 2), scalar2=zero[:, 0:1], op0=ALU.mult, op1=ALU.add,
-            )
+            for cubic, last_read in ((DEN, AT_TURN_DEN), (NUM, AT_TURN_NUM)):
+                affine_sb[t, cubic] = work.tile(
+                    [P, HALF], F32, name="affine%d" % cubic, bufs=sbuf_slots(AT_AFFINE, last_read)
+                )
+                nc.gpsimd.tensor_scalar(
+                    out=affine_sb[t, cubic][:], in0=y2_sb[t][:],
+                    scalar1=slope[:, cubic, g, ot : ot + 1], scalar2=offset[:, cubic, g, ot : ot + 1],
+                    op0=ALU.mult, op1=ALU.add,
+                )
 
         def product(t):
-            pan, ot, g = where(t)
-            prod_sb[t] = work.tile([P, 2, HALF], F32, name="prod", bufs=sbuf_slots(AT_PRODUCT, AT_TURN_NUM))
-            nc.vector.scalar_tensor_tensor(
-                out=prod_sb[t][:], in0=s_ps[t][:].unsqueeze(1).to_broadcast([P, 2, HALF]),
-                scalar=column(b_cols, OUT_TILES, g, ot), in1=inner_sb[t][:], op0=ALU.add, op1=ALU.mult,
-            )
+            g = where(t)[2]
+            for cubic, last_read in ((DEN, AT_TURN_DEN), (NUM, AT_TURN_NUM)):
+                prod_sb[t, cubic] = work.tile(
+                    [P, HALF], F32, name="prod%d" % cubic, bufs=sbuf_slots(AT_PRODUCT, last_read)
+                )
+                nc.vector.scalar_tensor_tensor(
+                    out=prod_sb[t, cubic][:], in0=y2_sb[t][:], scalar=linear[:, cubic, g : g + 1], in1=s_ps[t][:],
+                    op0=ALU.add, op1=ALU.mult,
+                )
+
+        def turn(out_ps, t, cubic, row_tiles):
+            for rt in row_tiles:
+                cols = slice(rt * P, (rt + 1) * P)
+                nc.tensor.matmul(
+                    out=out_ps[:, rt, :], lhsT=affine_sb[t, cubic][:, cols], rhs=ident[:],
+                    is_transpose=True, start=True, stop=False,
+                )
+                nc.tensor.matmul(
+                    out=out_ps[:, rt, :], lhsT=prod_sb[t, cubic][:, cols], rhs=ident[:],
+                    is_transpose=True, start=False, stop=True,
+                )
 
         def turn_den(t):
             den_ps[t] = psum.tile([P, ROW_TILES, P], F32, name="den_ps", bufs=psum_banks(AT_TURN_DEN, AT_ABS))
-            for rt in range(ROW_TILES):
-                nc.tensor.transpose(den_ps[t][:, rt, :], prod_sb[t][:, DEN, rt * P : (rt + 1) * P], ident[:])
+            turn(den_ps[t], t, DEN, range(ROW_TILES))
 
         def turn_num(t, row_tiles):
             if t not in num_ps:
                 num_ps[t] = psum.tile([P, ROW_TILES, P], F32, name="num_ps", bufs=psum_banks(AT_TURN_NUM, AT_FINISH))
-            for rt in row_tiles:
-                cols = slice(rt * P, (rt + 1) * P)
-                if rt in blocks_by_matmul(t // PAIR):
-                    nc.tensor.matmul(
-                        out=num_ps[t][:, rt, :], lhsT=y2_sb[t // PAIR][:, t % PAIR, cols],
-                        rhs=p2_diag[:, where(t)[2], :], start=True, stop=False,
-                    )
-                else:
-                    nc.tensor.matmul(
-                        out=num_ps[t][:, rt, :], lhsT=outer_sb[t // PAIR][:, t % PAIR, cols], rhs=ident[:],
-                        is_transpose=True, start=True, stop=False,
-                    )
-                nc.tensor.matmul(
-                    out=num_ps[t][:, rt, :], lhsT=prod_sb[t][:, NUM, cols], rhs=ident[:],
-                    is_transpose=True, start=False, stop=True,
-                )
+            turn(num_ps[t], t, NUM, row_tiles)
 
         def absolute(t):
             a_sb[t] = work.tile([P, ROW_TILES, P], F32, name="a", bufs=sbuf_slots(AT_ABS, AT_ROOT))
-            nc.scalar.activation(out=a_sb[t][:], in_=den_ps[t][:], func=ACT.Abs)
+            nc.scalar.activation(
+                out=a_sb[t][:], in_=den_ps[t][:], func=ACT.Abs, scale=leading[:, DEN, where(t)[2] : where(t)[2] + 1]
+            )
 
         def root(t):
             u_sb[t] = work.tile([P, ROW_TILES, P], F32, name="u", bufs=sbuf_slots(AT_ROOT, AT_SQUARE))
@@ -217,8 +191,8 @@ def tile_groupkanlayer_e_kernel(tc, x, W_words, W_scales, b, p, q, out):
             pan, ot, g = where(t)
             out_sb = work.tile([P, ROW_TILES, P], F32, name="out_sb", bufs=STORE_BUFS)
             nc.vector.scalar_tensor_tensor(
-                out=out_sb[:], in0=num_ps[t][:], scalar=column(p_f32, P_COEFS, g, 0), in1=r_sb[t][:],
-                op0=ALU.add, op1=ALU.mult,
+                out=out_sb[:], in0=num_ps[t][:], scalar=leading[:, NUM, g : g + 1], in1=r_sb[t][:],
+                op0=ALU.mult, op1=ALU.mult,
             )
             row0, col0 = pan % HALVES * HALF, g * GOUT + ot * P
             nc.sync.dma_start(
@@ -255,30 +229,55 @@ def tile_groupkanlayer_e_kernel(tc, x, W_words, W_scales, b, p, q, out):
         nc.scalar.dma_start(out=q_bf[:], in_=q.rearrange("g i -> (g i)").partition_broadcast(P))
         one = const.tile([P, 1], F32)
         nc.vector.memset(one[:], 1.0)
-        zero = const.tile([P, 1], F32)
-        nc.vector.memset(zero[:], 0.0)
 
         nc.vector.tensor_copy(out=b_rows[0 : GROUPS * OUT_TILES, :], in_=b_bf[:])
         b_turned = psum.tile([P, HALF], F32, name="s_ps", bufs=psum_banks(AT_MULTIPLY, AT_PRODUCT))
         nc.tensor.transpose(b_turned[:, 0:P], b_rows[:], ident[:])
         b_cols = const.tile([P, GROUPS * OUT_TILES], F32)
         nc.vector.tensor_copy(out=b_cols[:], in_=b_turned[:, 0 : GROUPS * OUT_TILES])
-        p_f32 = const.tile([P, GROUPS * P_COEFS], F32)
-        q_f32 = const.tile([P, GROUPS * Q_COEFS], F32)
-        nc.vector.tensor_copy(out=p_f32[:], in_=p_bf[:])
-        nc.vector.tensor_copy(out=q_f32[:], in_=q_bf[:])
-        p2_diag = const.tile([P, GROUPS, P], F32)
-        for g in range(GROUPS):
-            nc.vector.tensor_scalar(
-                out=p2_diag[:, g, :], in0=ident[:], scalar1=column(p_f32, P_COEFS, g, 2), scalar2=None, op0=ALU.mult,
+        p_of = p_bf[:].rearrange("p (g i) -> p g i", i=P_COEFS)
+        q_of = q_bf[:].rearrange("p (g i) -> p g i", i=Q_COEFS)
+        leading = const.tile([P, 2, GROUPS], F32)
+        sign = const.tile([P, 2, GROUPS], F32)
+        inverse = const.tile([P, 2, GROUPS], F32)
+        nc.vector.tensor_copy(out=leading[:, NUM, :], in_=p_of[:, :, 3])
+        nc.vector.tensor_copy(out=leading[:, DEN, :], in_=q_of[:, :, 2])
+        nc.vector.tensor_scalar(
+            out=sign[:], in0=leading[:], scalar1=0.0, scalar2=2.0, op0=ALU.is_ge, op1=ALU.mult
+        )
+        nc.vector.tensor_scalar(out=sign[:], in0=sign[:], scalar1=-1.0, scalar2=None, op0=ALU.add)
+        nc.vector.tensor_tensor(out=leading[:], in0=leading[:], in1=sign[:], op=ALU.mult)
+        nc.vector.scalar_tensor_tensor(
+            out=leading[:], in0=leading[:], scalar=TINY, in1=sign[:], op0=ALU.max, op1=ALU.mult
+        )
+        nc.vector.reciprocal(out=inverse[:], in_=leading[:])
+        linear = const.tile([P, 2, GROUPS], F32)
+        square_term = const.tile([P, 2, GROUPS], F32)
+        constant = const.tile([P, GROUPS], F32)
+        for cubic, coefs, i in ((NUM, p_of, 1), (DEN, q_of, 0)):
+            nc.vector.tensor_tensor(
+                out=linear[:, cubic, :], in0=coefs[:, :, i], in1=inverse[:, cubic, :], op=ALU.mult
             )
-        k_cols = const.tile([P, GROUPS * OUT_TILES], F32)
-        for g in range(GROUPS):
-            nc.vector.tensor_scalar(
-                out=k_cols[:, OUT_TILES * g : OUT_TILES * (g + 1)], in0=b_cols[:, OUT_TILES * g : OUT_TILES * (g + 1)],
-                scalar1=column(q_f32, Q_COEFS, g, 1), scalar2=column(q_f32, Q_COEFS, g, 0),
-                op0=ALU.mult, op1=ALU.add,
+            nc.vector.tensor_tensor(
+                out=square_term[:, cubic, :], in0=coefs[:, :, i + 1], in1=inverse[:, cubic, :], op=ALU.mult
             )
+        nc.vector.tensor_tensor(out=constant[:], in0=p_of[:, :, 0], in1=inverse[:, NUM, :], op=ALU.mult)
+        b_of = b_cols[:].rearrange("p (g ot) -> p g ot", ot=OUT_TILES)
+        slope = const.tile([P, 2, GROUPS, OUT_TILES], F32)
+        offset = const.tile([P, 2, GROUPS, OUT_TILES], F32)
+        for cubic in (DEN, NUM):
+            nc.vector.tensor_tensor(
+                out=slope[:, cubic], in0=b_of,
+                in1=square_term[:, cubic, :].unsqueeze(2).to_broadcast([P, GROUPS, OUT_TILES]), op=ALU.add,
+            )
+            nc.vector.tensor_tensor(
+                out=offset[:, cubic], in0=b_of,
+                in1=linear[:, cubic, :].unsqueeze(2).to_broadcast([P, GROUPS, OUT_TILES]), op=ALU.mult,
+            )
+        nc.vector.tensor_tensor(
+            out=offset[:, NUM], in0=offset[:, NUM],
+            in1=constant[:].unsqueeze(2).to_broadcast([P, GROUPS, OUT_TILES]), op=ALU.add,
+        )
 
         def run(stage, step, at, count):
             if 0 <= step - at < count:
@@ -291,10 +290,9 @@ def tile_groupkanlayer_e_kernel(tc, x, W_words, W_scales, b, p, q, out):
         for step in range(AT_TURN_X, TILES + AT_FINISH):
             run(load_x, step, AT_LOAD, PIECES)
 
-            run(inner_den, step, AT_INNER_DEN, TILES)
-            run(finish, step, AT_FINISH, TILES)
-            run(product, step, AT_PRODUCT, TILES)
             run(lambda j: group_x(j, True), step, AT_GROUP_X, PIECES)
+            run(product, step, AT_PRODUCT, TILES)
+            run(finish, step, AT_FINISH, TILES)
             run(quantise_if_complete, step, AT_QUANTISE, PIECES)
 
             run(square_y, step, AT_SQUARE_Y, TILES)
@@ -303,8 +301,7 @@ def tile_groupkanlayer_e_kernel(tc, x, W_words, W_scales, b, p, q, out):
             run(root, step, AT_ROOT, TILES)
             run(square, step, AT_SQUARE, TILES)
 
-            run(outer_num, step, AT_OUTER_NUM, TILES)
-            run(inner, step, AT_INNER, TILES)
+            run(affine, step, AT_AFFINE, TILES)
 
             run(lambda t: turn_num(t, range(0, ROW_TILES // 2)), step, AT_TURN_NUM, TILES)
             run(turn_den, step, AT_TURN_DEN, TILES)

@@ -28,13 +28,15 @@ PIECES = PANELS * ROW_TILES
 NUM, DEN = 0, 1
 P_COEFS, Q_COEFS = 4, 3
 
-AT_LOAD, AT_TURN_X, AT_GROUP_X, AT_QUANTISE = -15, -7, -6, -5
-AT_MULTIPLY, AT_SQUARE_Y, AT_PRODUCT, AT_AFFINE, AT_TURN_DEN = -1, 0, 1, 1, 2
-AT_ABS, AT_ROOT, AT_SQUARE, AT_TURN_NUM, AT_FINISH = 3, 4, 5, 5, 6
+AT_LOAD, AT_TURN_X, AT_GROUP_X, AT_QUANTISE = -15, -7, -5, -4
+AT_MULTIPLY, AT_SQUARE_Y, AT_AFFINE, AT_PRODUCT, AT_TURN_DEN = -1, 0, 0, 1, 2
+AT_ABS, AT_ROOT, AT_SQUARE, AT_TURN_NUM, AT_FINISH = 3, 3, 4, 3, 4
+GPSIMD_SQUARES = 4
+
 TINY = 2.0**-60
 
 PANEL_BUFS = 2
-STORE_BUFS = 3
+STORE_BUFS = 5
 
 FLOPS = 2 * ROWS * GROUPS * GIN * GOUT
 
@@ -73,9 +75,9 @@ def tile_groupkanlayer_e_kernel(tc, x, W_words, W_scales, b, p, q, out):
             elif j < ROW_TILES:
                 x_turned[j] = psum.tile([P, 2, P], F32, name="num_ps", bufs=psum_banks(AT_TURN_NUM, AT_FINISH))
             elif j == ROW_TILES:
-                x_turned[j] = psum.tile([P, 2, P], F32, name="s_ps", bufs=psum_banks(AT_MULTIPLY, AT_PRODUCT))
+                x_turned[j] = psum.tile([P, 2, P], F32, name="s_ps", bufs=2)
             else:
-                x_turned[j] = psum.tile([P, 2, P], F32, name="x_turned", bufs=1)
+                x_turned[j] = psum.tile([P, 2, P], F32, name="x_turned", bufs=2)
             for w in range(2):
                 nc.tensor.transpose(x_turned[j][:, w, :], words[:, w : GIN // 2 : 2], ident[:])
 
@@ -109,7 +111,7 @@ def tile_groupkanlayer_e_kernel(tc, x, W_words, W_scales, b, p, q, out):
         def multiply(t):
             pan, ot, g = where(t)
             if t not in s_ps:
-                s_ps[t] = psum.tile([P, HALF], F32, name="s_ps", bufs=psum_banks(AT_MULTIPLY, AT_PRODUCT))
+                s_ps[t] = psum.tile([P, HALF], F32, name="s_ps", bufs=2)
             nc.tensor.matmul_mx(
                 out=s_ps[t][:],
                 lhsT=w_words[:, g, 2 * P * ot : 2 * P * (ot + 1)].bitcast(FP4X4),
@@ -127,28 +129,28 @@ def tile_groupkanlayer_e_kernel(tc, x, W_words, W_scales, b, p, q, out):
                 out=y2_sb[t][:], in_=s_ps[t][:], func=ACT.Square, bias=column(b_cols, OUT_TILES, g, ot), scale=1.0,
             )
 
-        def affine(t):
+        def affine(t, cubic):
             pan, ot, g = where(t)
-            for cubic, last_read in ((DEN, AT_TURN_DEN), (NUM, AT_TURN_NUM)):
-                affine_sb[t, cubic] = work.tile(
-                    [P, HALF], F32, name="affine%d" % cubic, bufs=sbuf_slots(AT_AFFINE, last_read)
-                )
-                nc.gpsimd.tensor_scalar(
-                    out=affine_sb[t, cubic][:], in0=y2_sb[t][:],
-                    scalar1=slope[:, cubic, g, ot : ot + 1], scalar2=offset[:, cubic, g, ot : ot + 1],
-                    op0=ALU.mult, op1=ALU.add,
-                )
+            last_read = (AT_TURN_NUM, AT_TURN_DEN)[cubic]
+            affine_sb[t, cubic] = work.tile(
+                [P, HALF], F32, name="affine%d" % cubic, bufs=sbuf_slots(AT_AFFINE, last_read)
+            )
+            nc.gpsimd.tensor_scalar(
+                out=affine_sb[t, cubic][:], in0=y2_sb[t][:],
+                scalar1=slope[:, cubic, g, ot : ot + 1], scalar2=offset[:, cubic, g, ot : ot + 1],
+                op0=ALU.mult, op1=ALU.add,
+            )
 
-        def product(t):
+        def product(t, cubic):
             g = where(t)[2]
-            for cubic, last_read in ((DEN, AT_TURN_DEN), (NUM, AT_TURN_NUM)):
-                prod_sb[t, cubic] = work.tile(
-                    [P, HALF], F32, name="prod%d" % cubic, bufs=sbuf_slots(AT_PRODUCT, last_read)
-                )
-                nc.vector.scalar_tensor_tensor(
-                    out=prod_sb[t, cubic][:], in0=y2_sb[t][:], scalar=linear[:, cubic, g : g + 1], in1=s_ps[t][:],
-                    op0=ALU.add, op1=ALU.mult,
-                )
+            last_read = (AT_TURN_NUM, AT_TURN_DEN)[cubic]
+            prod_sb[t, cubic] = work.tile(
+                [P, HALF], F32, name="prod%d" % cubic, bufs=sbuf_slots(AT_PRODUCT, last_read)
+            )
+            nc.vector.scalar_tensor_tensor(
+                out=prod_sb[t, cubic][:], in0=y2_sb[t][:], scalar=linear[:, cubic, g : g + 1], in1=s_ps[t][:],
+                op0=ALU.add, op1=ALU.mult,
+            )
 
         def turn(out_ps, t, cubic, row_tiles):
             for rt in row_tiles:
@@ -173,19 +175,23 @@ def tile_groupkanlayer_e_kernel(tc, x, W_words, W_scales, b, p, q, out):
 
         def absolute(t):
             a_sb[t] = work.tile([P, ROW_TILES, P], F32, name="a", bufs=sbuf_slots(AT_ABS, AT_ROOT))
-            nc.scalar.activation(
-                out=a_sb[t][:], in_=den_ps[t][:], func=ACT.Abs, scale=leading[:, DEN, where(t)[2] : where(t)[2] + 1]
-            )
+            nc.scalar.activation(out=a_sb[t][:], in_=den_ps[t][:], func=ACT.Abs)
 
         def root(t):
             u_sb[t] = work.tile([P, ROW_TILES, P], F32, name="u", bufs=sbuf_slots(AT_ROOT, AT_SQUARE))
             nc.scalar.activation(
-                out=u_sb[t][:], in_=a_sb[t][:], func=ACT.Abs_reciprocal_sqrt, bias=one[:, 0:1], scale=1.0
+                out=u_sb[t][:], in_=a_sb[t][:], func=ACT.Abs_reciprocal_sqrt, bias=one[:, 0:1],
+                scale=magnitude[:, DEN, where(t)[2] : where(t)[2] + 1],
             )
 
-        def square(t):
-            r_sb[t] = work.tile([P, ROW_TILES, P], F32, name="r", bufs=sbuf_slots(AT_SQUARE, AT_FINISH))
-            nc.scalar.activation(out=r_sb[t][:], in_=u_sb[t][:], func=ACT.Square)
+        def square(t, by_gpsimd):
+            if by_gpsimd != (t % GPSIMD_SQUARES == GPSIMD_SQUARES - 1):
+                return
+            r_sb[t] = work.tile([P, ROW_TILES, P], F32, name="r", bufs=sbuf_slots(AT_ROOT, AT_FINISH))
+            if by_gpsimd:
+                nc.gpsimd.tensor_tensor(out=r_sb[t][:], in0=u_sb[t][:], in1=u_sb[t][:], op=ALU.mult)
+            else:
+                nc.scalar.activation(out=r_sb[t][:], in_=u_sb[t][:], func=ACT.Square)
 
         def finish(t):
             pan, ot, g = where(t)
@@ -231,7 +237,7 @@ def tile_groupkanlayer_e_kernel(tc, x, W_words, W_scales, b, p, q, out):
         nc.vector.memset(one[:], 1.0)
 
         nc.vector.tensor_copy(out=b_rows[0 : GROUPS * OUT_TILES, :], in_=b_bf[:])
-        b_turned = psum.tile([P, HALF], F32, name="s_ps", bufs=psum_banks(AT_MULTIPLY, AT_PRODUCT))
+        b_turned = psum.tile([P, HALF], F32, name="s_ps", bufs=2)
         nc.tensor.transpose(b_turned[:, 0:P], b_rows[:], ident[:])
         b_cols = const.tile([P, GROUPS * OUT_TILES], F32)
         nc.vector.tensor_copy(out=b_cols[:], in_=b_turned[:, 0 : GROUPS * OUT_TILES])
@@ -246,10 +252,10 @@ def tile_groupkanlayer_e_kernel(tc, x, W_words, W_scales, b, p, q, out):
             out=sign[:], in0=leading[:], scalar1=0.0, scalar2=2.0, op0=ALU.is_ge, op1=ALU.mult
         )
         nc.vector.tensor_scalar(out=sign[:], in0=sign[:], scalar1=-1.0, scalar2=None, op0=ALU.add)
-        nc.vector.tensor_tensor(out=leading[:], in0=leading[:], in1=sign[:], op=ALU.mult)
-        nc.vector.scalar_tensor_tensor(
-            out=leading[:], in0=leading[:], scalar=TINY, in1=sign[:], op0=ALU.max, op1=ALU.mult
-        )
+        magnitude = const.tile([P, 2, GROUPS], F32)
+        nc.vector.tensor_tensor(out=magnitude[:], in0=leading[:], in1=sign[:], op=ALU.mult)
+        nc.vector.tensor_scalar(out=magnitude[:], in0=magnitude[:], scalar1=TINY, scalar2=None, op0=ALU.max)
+        nc.vector.tensor_tensor(out=leading[:], in0=magnitude[:], in1=sign[:], op=ALU.mult)
         nc.vector.reciprocal(out=inverse[:], in_=leading[:])
         linear = const.tile([P, 2, GROUPS], F32)
         square_term = const.tile([P, 2, GROUPS], F32)
@@ -289,22 +295,20 @@ def tile_groupkanlayer_e_kernel(tc, x, W_words, W_scales, b, p, q, out):
 
         for step in range(AT_TURN_X, TILES + AT_FINISH):
             run(load_x, step, AT_LOAD, PIECES)
-
-            run(lambda j: group_x(j, True), step, AT_GROUP_X, PIECES)
-            run(product, step, AT_PRODUCT, TILES)
-            run(finish, step, AT_FINISH, TILES)
-            run(quantise_if_complete, step, AT_QUANTISE, PIECES)
-
-            run(square_y, step, AT_SQUARE_Y, TILES)
-            run(lambda j: group_x(j, False), step, AT_GROUP_X, PIECES)
             run(absolute, step, AT_ABS, TILES)
+            run(lambda t: square(t, False), step, AT_SQUARE, TILES)
+            run(square_y, step, AT_SQUARE_Y, TILES)
             run(root, step, AT_ROOT, TILES)
-            run(square, step, AT_SQUARE, TILES)
-
-            run(affine, step, AT_AFFINE, TILES)
-
-            run(lambda t: turn_num(t, range(0, ROW_TILES // 2)), step, AT_TURN_NUM, TILES)
+            run(lambda j: group_x(j, False), step, AT_GROUP_X, PIECES)
+            run(lambda t: affine(t, DEN), step, AT_AFFINE, TILES)
+            run(lambda t: square(t, True), step, AT_ROOT, TILES)
+            run(lambda t: affine(t, NUM), step, AT_AFFINE, TILES)
+            run(lambda t: product(t, DEN), step, AT_PRODUCT, TILES)
+            run(lambda t: product(t, NUM), step, AT_PRODUCT, TILES)
+            run(quantise_if_complete, step, AT_QUANTISE, PIECES)
+            run(lambda j: group_x(j, True), step, AT_GROUP_X, PIECES)
+            run(finish, step, AT_FINISH, TILES)
             run(turn_den, step, AT_TURN_DEN, TILES)
+            run(lambda t: turn_num(t, range(ROW_TILES)), step, AT_TURN_NUM, TILES)
             run(multiply, step, AT_MULTIPLY, TILES)
-            run(lambda t: turn_num(t, range(ROW_TILES // 2, ROW_TILES)), step, AT_TURN_NUM, TILES)
             run(turn_x, step, AT_TURN_X, PIECES)

@@ -28,10 +28,11 @@ PIECES = PANELS * ROW_TILES
 NUM, DEN = 0, 1
 P_COEFS, Q_COEFS = 4, 3
 
-AT_LOAD, AT_TURN_X, AT_GROUP_X, AT_QUANTISE = -15, -7, -5, -4
+AT_LOAD, AT_TURN_X, AT_GROUP_X, AT_QUANTISE = -16, -8, -6, -5
 AT_MULTIPLY, AT_SQUARE_Y, AT_AFFINE, AT_PRODUCT, AT_TURN_DEN = -1, 0, 0, 1, 2
 AT_ABS, AT_ROOT, AT_SQUARE, AT_TURN_NUM, AT_FINISH = 3, 3, 4, 3, 4
 GPSIMD_SQUARES = 4
+VECTOR_SQUARES = 3
 
 TINY = 2.0**-60
 
@@ -82,7 +83,7 @@ def tile_groupkanlayer_e_kernel(tc, x, W_words, W_scales, b, p, q, out):
                 nc.tensor.transpose(x_turned[j][:, w, :], words[:, w : GIN // 2 : 2], ident[:])
 
         def group_x(j, by_vector):
-            if by_vector == (j < ROW_TILES and j % 2 == 0):
+            if by_vector != (not (j < ROW_TILES and j % 2 == 0 or ROW_TILES <= j < 2 * ROW_TILES)):
                 return
             pan, rt = divmod(j, ROW_TILES)
             if rt == 0:
@@ -184,12 +185,18 @@ def tile_groupkanlayer_e_kernel(tc, x, W_words, W_scales, b, p, q, out):
                 scale=magnitude[:, DEN, where(t)[2] : where(t)[2] + 1],
             )
 
-        def square(t, by_gpsimd):
-            if by_gpsimd != (t % GPSIMD_SQUARES == GPSIMD_SQUARES - 1):
+        def square(t, engine):
+            if t >= TILES - VECTOR_SQUARES:
+                owner = nc.vector
+            elif t % GPSIMD_SQUARES == GPSIMD_SQUARES - 1:
+                owner = nc.gpsimd
+            else:
+                owner = nc.scalar
+            if engine is not owner:
                 return
             r_sb[t] = work.tile([P, ROW_TILES, P], F32, name="r", bufs=sbuf_slots(AT_ROOT, AT_FINISH))
-            if by_gpsimd:
-                nc.gpsimd.tensor_tensor(out=r_sb[t][:], in0=u_sb[t][:], in1=u_sb[t][:], op=ALU.mult)
+            if engine is not nc.scalar:
+                engine.tensor_tensor(out=r_sb[t][:], in0=u_sb[t][:], in1=u_sb[t][:], op=ALU.mult)
             else:
                 nc.scalar.activation(out=r_sb[t][:], in_=u_sb[t][:], func=ACT.Square)
 
@@ -244,46 +251,55 @@ def tile_groupkanlayer_e_kernel(tc, x, W_words, W_scales, b, p, q, out):
         p_of = p_bf[:].rearrange("p (g i) -> p g i", i=P_COEFS)
         q_of = q_bf[:].rearrange("p (g i) -> p g i", i=Q_COEFS)
         leading = const.tile([P, 2, GROUPS], F32)
-        sign = const.tile([P, 2, GROUPS], F32)
+        magnitude = const.tile([P, 2, GROUPS], F32)
+        too_small = const.tile([P, 2, GROUPS], F32)
         inverse = const.tile([P, 2, GROUPS], F32)
         nc.vector.tensor_copy(out=leading[:, NUM, :], in_=p_of[:, :, 3])
         nc.vector.tensor_copy(out=leading[:, DEN, :], in_=q_of[:, :, 2])
+
+        def absolute_value(out_tile, in_tile):
+            nc.vector.scalar_tensor_tensor(
+                out=out_tile[:], in0=in_tile[:], scalar=-1.0, in1=in_tile[:], op0=ALU.mult, op1=ALU.max
+            )
+
+        absolute_value(magnitude, leading)
         nc.vector.tensor_scalar(
-            out=sign[:], in0=leading[:], scalar1=0.0, scalar2=2.0, op0=ALU.is_ge, op1=ALU.mult
+            out=too_small[:], in0=magnitude[:], scalar1=TINY, scalar2=2.0 * TINY, op0=ALU.is_lt, op1=ALU.mult
         )
-        nc.vector.tensor_scalar(out=sign[:], in0=sign[:], scalar1=-1.0, scalar2=None, op0=ALU.add)
-        magnitude = const.tile([P, 2, GROUPS], F32)
-        nc.vector.tensor_tensor(out=magnitude[:], in0=leading[:], in1=sign[:], op=ALU.mult)
-        nc.vector.tensor_scalar(out=magnitude[:], in0=magnitude[:], scalar1=TINY, scalar2=None, op0=ALU.max)
-        nc.vector.tensor_tensor(out=leading[:], in0=magnitude[:], in1=sign[:], op=ALU.mult)
+        nc.vector.tensor_tensor(out=leading[:], in0=leading[:], in1=too_small[:], op=ALU.add)
         nc.vector.reciprocal(out=inverse[:], in_=leading[:])
+
         linear = const.tile([P, 2, GROUPS], F32)
         square_term = const.tile([P, 2, GROUPS], F32)
         constant = const.tile([P, GROUPS], F32)
-        for cubic, coefs, i in ((NUM, p_of, 1), (DEN, q_of, 0)):
-            nc.vector.tensor_tensor(
-                out=linear[:, cubic, :], in0=coefs[:, :, i], in1=inverse[:, cubic, :], op=ALU.mult
-            )
-            nc.vector.tensor_tensor(
-                out=square_term[:, cubic, :], in0=coefs[:, :, i + 1], in1=inverse[:, cubic, :], op=ALU.mult
-            )
-        nc.vector.tensor_tensor(out=constant[:], in0=p_of[:, :, 0], in1=inverse[:, NUM, :], op=ALU.mult)
-        b_of = b_cols[:].rearrange("p (g ot) -> p g ot", ot=OUT_TILES)
         slope = const.tile([P, 2, GROUPS, OUT_TILES], F32)
         offset = const.tile([P, 2, GROUPS, OUT_TILES], F32)
-        for cubic in (DEN, NUM):
+
+        def make_tables():
+            for cubic, coefs, i in ((DEN, q_of, 0), (NUM, p_of, 1)):
+                nc.vector.tensor_tensor(
+                    out=linear[:, cubic, :], in0=coefs[:, :, i], in1=inverse[:, cubic, :], op=ALU.mult
+                )
+                nc.vector.tensor_tensor(
+                    out=square_term[:, cubic, :], in0=coefs[:, :, i + 1], in1=inverse[:, cubic, :], op=ALU.mult
+                )
+            nc.vector.tensor_tensor(out=constant[:], in0=p_of[:, :, 0], in1=inverse[:, NUM, :], op=ALU.mult)
+            b_of = b_cols[:].rearrange("p (g ot) -> p g ot", ot=OUT_TILES)
+
+            def per_tile(table):
+                return table.unsqueeze(2).to_broadcast([P, GROUPS, OUT_TILES])
+
+            for cubic in (DEN, NUM):
+                nc.vector.tensor_tensor(
+                    out=slope[:, cubic], in0=b_of, in1=per_tile(square_term[:, cubic, :]), op=ALU.add
+                )
+                nc.vector.tensor_tensor(
+                    out=offset[:, cubic], in0=b_of, in1=per_tile(linear[:, cubic, :]), op=ALU.mult
+                )
             nc.vector.tensor_tensor(
-                out=slope[:, cubic], in0=b_of,
-                in1=square_term[:, cubic, :].unsqueeze(2).to_broadcast([P, GROUPS, OUT_TILES]), op=ALU.add,
+                out=offset[:, NUM], in0=offset[:, NUM], in1=per_tile(constant[:]), op=ALU.add
             )
-            nc.vector.tensor_tensor(
-                out=offset[:, cubic], in0=b_of,
-                in1=linear[:, cubic, :].unsqueeze(2).to_broadcast([P, GROUPS, OUT_TILES]), op=ALU.mult,
-            )
-        nc.vector.tensor_tensor(
-            out=offset[:, NUM], in0=offset[:, NUM],
-            in1=constant[:].unsqueeze(2).to_broadcast([P, GROUPS, OUT_TILES]), op=ALU.add,
-        )
+            absolute_value(magnitude, leading)
 
         def run(stage, step, at, count):
             if 0 <= step - at < count:
@@ -296,17 +312,20 @@ def tile_groupkanlayer_e_kernel(tc, x, W_words, W_scales, b, p, q, out):
         for step in range(AT_TURN_X, TILES + AT_FINISH):
             run(load_x, step, AT_LOAD, PIECES)
             run(absolute, step, AT_ABS, TILES)
-            run(lambda t: square(t, False), step, AT_SQUARE, TILES)
+            run(lambda t: square(t, nc.scalar), step, AT_SQUARE, TILES)
             run(square_y, step, AT_SQUARE_Y, TILES)
             run(root, step, AT_ROOT, TILES)
             run(lambda j: group_x(j, False), step, AT_GROUP_X, PIECES)
             run(lambda t: affine(t, DEN), step, AT_AFFINE, TILES)
-            run(lambda t: square(t, True), step, AT_ROOT, TILES)
+            run(lambda t: square(t, nc.gpsimd), step, AT_ROOT, TILES)
             run(lambda t: affine(t, NUM), step, AT_AFFINE, TILES)
             run(lambda t: product(t, DEN), step, AT_PRODUCT, TILES)
             run(lambda t: product(t, NUM), step, AT_PRODUCT, TILES)
             run(quantise_if_complete, step, AT_QUANTISE, PIECES)
+            if step == AT_QUANTISE + ROW_TILES - 1:
+                make_tables()
             run(lambda j: group_x(j, True), step, AT_GROUP_X, PIECES)
+            run(lambda t: square(t, nc.vector), step, AT_SQUARE, TILES)
             run(finish, step, AT_FINISH, TILES)
             run(turn_den, step, AT_TURN_DEN, TILES)
             run(lambda t: turn_num(t, range(ROW_TILES)), step, AT_TURN_NUM, TILES)

from contextlib import ExitStack

import concourse.mybir as mybir
from concourse.masks import make_identity

F32 = mybir.dt.float32
BF16 = mybir.dt.bfloat16
I32 = mybir.dt.int32
U8 = mybir.dt.uint8
U32 = mybir.dt.uint32
FP8X4 = mybir.dt.float8_e4m3fn_x4
FP4X4 = mybir.dt.float4_e2m1fn_x4
ACT = mybir.ActivationFunctionType
ALU = mybir.AluOpType

P = 128
ROWS = 1024
GROUPS = 8
GIN = 512
GOUT = 512
HALF = 512
HALVES = ROWS // HALF
ROW_TILES = HALF // P
OUT_TILES = GOUT // P
PANELS = GROUPS * HALVES
TILES = PANELS * OUT_TILES
PIECES = PANELS * ROW_TILES
NUM, DEN = 0, 1
P_COEFS, Q_COEFS = 4, 3

AT_LOAD, AT_TURN_X, AT_GROUP_X, AT_QUANTISE = -16, -8, -6, -5
AT_MULTIPLY, AT_SQUARE_Y, AT_AFFINE, AT_PRODUCT, AT_TURN_DEN = -1, 0, 0, 1, 2
AT_ABS, AT_ROOT, AT_SQUARE, AT_TURN_NUM, AT_FINISH = 3, 3, 4, 3, 4
GPSIMD_SQUARES = 4
VECTOR_SQUARES = 3

TINY = 2.0**-60

PANEL_BUFS = 2
STORE_BUFS = 5

FLOPS = 2 * ROWS * GROUPS * GIN * GOUT


def sbuf_slots(at_write, at_last_read):
    return at_last_read - at_write + 2


def psum_banks(at_write, at_last_read):
    return at_last_read - at_write + 1


def tile_groupkanlayer_e_kernel(tc, x, W_words, W_scales, b, p, q, out):
    nc = tc.nc
    with ExitStack() as ctx:
        const = ctx.enter_context(tc.tile_pool(name="const", bufs=1))
        work = ctx.enter_context(tc.tile_pool(name="work", bufs=2))
        psum = ctx.enter_context(tc.psum_pool(name="psum", bufs=2))
        ctx.enter_context(tc.manual_schedule())

        x_rows, x_turned, x_grouped, x_codes, x_scales = {}, {}, {}, {}, {}
        s_ps, y2_sb, affine_sb, prod_sb = {}, {}, {}, {}
        den_ps, num_ps, a_sb, u_sb, r_sb = {}, {}, {}, {}, {}

        def load_x(j):
            pan, rt = divmod(j, ROW_TILES)
            g, half = divmod(pan, HALVES)
            row0 = half * HALF + rt * P
            x_rows[j] = work.tile([P, GIN], BF16, name="x_rows", bufs=sbuf_slots(AT_LOAD, AT_TURN_X))
            nc.sync.dma_start(out=x_rows[j][:], in_=x[row0 : row0 + P, g * GIN : (g + 1) * GIN])

        def turn_x(j):
            words = x_rows[j][:].bitcast(F32)
            if j < ROW_TILES // 2:
                x_turned[j] = psum.tile([P, 2, P], F32, name="den_ps", bufs=psum_banks(AT_TURN_DEN, AT_ABS))
            elif j < ROW_TILES:
                x_turned[j] = psum.tile([P, 2, P], F32, name="num_ps", bufs=psum_banks(AT_TURN_NUM, AT_FINISH))
            elif j == ROW_TILES:
                x_turned[j] = psum.tile([P, 2, P], F32, name="s_ps", bufs=2)
            else:
                x_turned[j] = psum.tile([P, 2, P], F32, name="x_turned", bufs=2)
            for w in range(2):
                nc.tensor.transpose(x_turned[j][:, w, :], words[:, w : GIN // 2 : 2], ident[:])

        def group_x(j, by_vector):
            if by_vector != (not (j < ROW_TILES and j % 2 == 0 or ROW_TILES <= j < 2 * ROW_TILES)):
                return
            pan, rt = divmod(j, ROW_TILES)
            if rt == 0:
                x_grouped[pan] = work.tile([P, 4 * HALF], BF16, name="x_grouped", bufs=PANEL_BUFS, align_bytes=64)
            dst = x_grouped[pan][:, 4 * P * rt : 4 * P * (rt + 1)].bitcast(F32).rearrange("pp (n w) -> pp n w", w=2)
            src = x_turned[j][:].rearrange("pp w n -> pp n w")
            if by_vector:
                nc.vector.tensor_copy(out=dst, in_=src)
            else:
                nc.scalar.copy(out=dst, in_=src)

        def quantise_x(pan):
            x_codes[pan] = work.tile([P, HALF], U32, name="x_codes", bufs=PANEL_BUFS, align_bytes=64)
            x_scales[pan] = work.tile([P, HALF], U8, name="x_scales", bufs=PANEL_BUFS, align_bytes=64)
            nc.vector.quantize_mx(
                out=x_codes[pan][:].bitcast(FP8X4), scales=x_scales[pan][:], in_=x_grouped[pan][:]
            )

        def where(t):
            pan, ot = divmod(t, OUT_TILES)
            return pan, ot, pan // HALVES

        def column(table, width, g, i):
            return table[:, width * g + i : width * g + i + 1]

        def multiply(t):
            pan, ot, g = where(t)
            if t not in s_ps:
                s_ps[t] = psum.tile([P, HALF], F32, name="s_ps", bufs=2)
            nc.tensor.matmul_mx(
                out=s_ps[t][:],
                lhsT=w_words[:, g, 2 * P * ot : 2 * P * (ot + 1)].bitcast(FP4X4),
                lhsT_scale=w_scales[:, g, P * ot : P * (ot + 1)],
                rhs=x_codes[pan][:].bitcast(FP8X4),
                rhs_scale=x_scales[pan][:],
                start=True,
                stop=True,
            )

        def square_y(t):
            pan, ot, g = where(t)
            y2_sb[t] = work.tile([P, HALF], F32, name="y2", bufs=sbuf_slots(AT_SQUARE_Y, AT_PRODUCT))
            nc.scalar.activation(
                out=y2_sb[t][:], in_=s_ps[t][:], func=ACT.Square, bias=column(b_cols, OUT_TILES, g, ot), scale=1.0,
            )

        def affine(t, cubic):
            pan, ot, g = where(t)
            last_read = (AT_TURN_NUM, AT_TURN_DEN)[cubic]
            affine_sb[t, cubic] = work.tile(
                [P, HALF], F32, name="affine%d" % cubic, bufs=sbuf_slots(AT_AFFINE, last_read)
            )
            nc.gpsimd.tensor_scalar(
                out=affine_sb[t, cubic][:], in0=y2_sb[t][:],
                scalar1=slope[:, cubic, g, ot : ot + 1], scalar2=offset[:, cubic, g, ot : ot + 1],
                op0=ALU.mult, op1=ALU.add,
            )

        def product(t, cubic):
            g = where(t)[2]
            last_read = (AT_TURN_NUM, AT_TURN_DEN)[cubic]
            prod_sb[t, cubic] = work.tile(
                [P, HALF], F32, name="prod%d" % cubic, bufs=sbuf_slots(AT_PRODUCT, last_read)
            )
            nc.vector.scalar_tensor_tensor(
                out=prod_sb[t, cubic][:], in0=y2_sb[t][:], scalar=linear[:, cubic, g : g + 1], in1=s_ps[t][:],
                op0=ALU.add, op1=ALU.mult,
            )

        def turn(out_ps, t, cubic, row_tiles):
            for rt in row_tiles:
                cols = slice(rt * P, (rt + 1) * P)
                nc.tensor.matmul(
                    out=out_ps[:, rt, :], lhsT=affine_sb[t, cubic][:, cols], rhs=ident[:],
                    is_transpose=True, start=True, stop=False,
                )
                nc.tensor.matmul(
                    out=out_ps[:, rt, :], lhsT=prod_sb[t, cubic][:, cols], rhs=ident[:],
                    is_transpose=True, start=False, stop=True,
                )

        def turn_den(t):
            den_ps[t] = psum.tile([P, ROW_TILES, P], F32, name="den_ps", bufs=psum_banks(AT_TURN_DEN, AT_ABS))
            turn(den_ps[t], t, DEN, range(ROW_TILES))

        def turn_num(t, row_tiles):
            if t not in num_ps:
                num_ps[t] = psum.tile([P, ROW_TILES, P], F32, name="num_ps", bufs=psum_banks(AT_TURN_NUM, AT_FINISH))
            turn(num_ps[t], t, NUM, row_tiles)

        def absolute(t):
            a_sb[t] = work.tile([P, ROW_TILES, P], F32, name="a", bufs=sbuf_slots(AT_ABS, AT_ROOT))
            nc.scalar.activation(out=a_sb[t][:], in_=den_ps[t][:], func=ACT.Abs)

        def root(t):
            u_sb[t] = work.tile([P, ROW_TILES, P], F32, name="u", bufs=sbuf_slots(AT_ROOT, AT_SQUARE))
            nc.scalar.activation(
                out=u_sb[t][:], in_=a_sb[t][:], func=ACT.Abs_reciprocal_sqrt, bias=one[:, 0:1],
                scale=magnitude[:, DEN, where(t)[2] : where(t)[2] + 1],
            )

        def square(t, engine):
            if t >= TILES - VECTOR_SQUARES:
                owner = nc.vector
            elif t % GPSIMD_SQUARES == GPSIMD_SQUARES - 1:
                owner = nc.gpsimd
            else:
                owner = nc.scalar
            if engine is not owner:
                return
            r_sb[t] = work.tile([P, ROW_TILES, P], F32, name="r", bufs=sbuf_slots(AT_ROOT, AT_FINISH))
            if engine is not nc.scalar:
                engine.tensor_tensor(out=r_sb[t][:], in0=u_sb[t][:], in1=u_sb[t][:], op=ALU.mult)
            else:
                nc.scalar.activation(out=r_sb[t][:], in_=u_sb[t][:], func=ACT.Square)

        def finish(t):
            pan, ot, g = where(t)
            out_sb = work.tile([P, ROW_TILES, P], F32, name="out_sb", bufs=STORE_BUFS)
            nc.vector.scalar_tensor_tensor(
                out=out_sb[:], in0=num_ps[t][:], scalar=leading[:, NUM, g : g + 1], in1=r_sb[t][:],
                op0=ALU.mult, op1=ALU.mult,
            )
            row0, col0 = pan % HALVES * HALF, g * GOUT + ot * P
            nc.sync.dma_start(
                out=out[row0 : row0 + HALF, col0 : col0 + P].rearrange("(rt n) o -> n rt o", n=P), in_=out_sb[:]
            )

        for j in range(ROW_TILES):
            load_x(j)

        b_bf = const.tile([GROUPS * OUT_TILES, P], BF16)
        nc.scalar.dma_start(out=b_bf[:], in_=b.rearrange("g (ot o) -> (g ot) o", o=P))
        b_rows = const.tile([P, P], F32)
        nc.vector.memset(b_rows[:], 0.0)
        ident = const.tile([P, P], F32)
        make_identity(nc, ident[:])

        w_scales = const.tile([P, GROUPS, GOUT], U8, align_bytes=64)
        nc.vector.memset(w_scales[:].bitcast(I32), 0)
        for c in range(4):
            nc.sync.dma_start(
                out=w_scales[32 * c : 32 * c + 4].bitcast(I32),
                in_=W_scales.bitcast(I32)[:, 4 * c : 4 * c + 4, :].rearrange("g i o -> i g o"),
            )
        w_words = const.tile([P, GROUPS, 2 * GOUT], U8, align_bytes=64)
        w_dram = W_words.bitcast(I32).rearrange("g pp o -> pp g o")
        nc.sync.dma_start(out=w_words[:, 0:1, :].bitcast(I32), in_=w_dram[:, 0:1, :])
        for j in range(ROW_TILES, AT_TURN_X - AT_LOAD):
            load_x(j)
        nc.sync.dma_start(out=w_words[:, 1:GROUPS, :].bitcast(I32), in_=w_dram[:, 1:GROUPS, :])

        p_bf = const.tile([P, GROUPS * P_COEFS], BF16)
        q_bf = const.tile([P, GROUPS * Q_COEFS], BF16)
        nc.scalar.dma_start(out=p_bf[:], in_=p.rearrange("g i -> (g i)").partition_broadcast(P))
        nc.scalar.dma_start(out=q_bf[:], in_=q.rearrange("g i -> (g i)").partition_broadcast(P))
        one = const.tile([P, 1], F32)
        nc.vector.memset(one[:], 1.0)

        nc.vector.tensor_copy(out=b_rows[0 : GROUPS * OUT_TILES, :], in_=b_bf[:])
        b_turned = psum.tile([P, HALF], F32, name="s_ps", bufs=2)
        nc.tensor.transpose(b_turned[:, 0:P], b_rows[:], ident[:])
        b_cols = const.tile([P, GROUPS * OUT_TILES], F32)
        nc.vector.tensor_copy(out=b_cols[:], in_=b_turned[:, 0 : GROUPS * OUT_TILES])
        p_of = p_bf[:].rearrange("p (g i) -> p g i", i=P_COEFS)
        q_of = q_bf[:].rearrange("p (g i) -> p g i", i=Q_COEFS)
        leading = const.tile([P, 2, GROUPS], F32)
        magnitude = const.tile([P, 2, GROUPS], F32)
        too_small = const.tile([P, 2, GROUPS], F32)
        inverse = const.tile([P, 2, GROUPS], F32)
        nc.vector.tensor_copy(out=leading[:, NUM, :], in_=p_of[:, :, 3])
        nc.vector.tensor_copy(out=leading[:, DEN, :], in_=q_of[:, :, 2])

        def absolute_value(out_tile, in_tile):
            nc.vector.scalar_tensor_tensor(
                out=out_tile[:], in0=in_tile[:], scalar=-1.0, in1=in_tile[:], op0=ALU.mult, op1=ALU.max
            )

        absolute_value(magnitude, leading)
        nc.vector.tensor_scalar(
            out=too_small[:], in0=magnitude[:], scalar1=TINY, scalar2=2.0 * TINY, op0=ALU.is_lt, op1=ALU.mult
        )
        nc.vector.tensor_tensor(out=leading[:], in0=leading[:], in1=too_small[:], op=ALU.add)
        nc.vector.reciprocal(out=inverse[:], in_=leading[:])

        linear = const.tile([P, 2, GROUPS], F32)
        square_term = const.tile([P, 2, GROUPS], F32)
        constant = const.tile([P, GROUPS], F32)
        slope = const.tile([P, 2, GROUPS, OUT_TILES], F32)
        offset = const.tile([P, 2, GROUPS, OUT_TILES], F32)

        def make_tables():
            for cubic, coefs, i in ((DEN, q_of, 0), (NUM, p_of, 1)):
                nc.vector.tensor_tensor(
                    out=linear[:, cubic, :], in0=coefs[:, :, i], in1=inverse[:, cubic, :], op=ALU.mult
                )
                nc.vector.tensor_tensor(
                    out=square_term[:, cubic, :], in0=coefs[:, :, i + 1], in1=inverse[:, cubic, :], op=ALU.mult
                )
            nc.vector.tensor_tensor(out=constant[:], in0=p_of[:, :, 0], in1=inverse[:, NUM, :], op=ALU.mult)
            b_of = b_cols[:].rearrange("p (g ot) -> p g ot", ot=OUT_TILES)

            def per_tile(table):
                return table.unsqueeze(2).to_broadcast([P, GROUPS, OUT_TILES])

            for cubic in (DEN, NUM):
                nc.vector.tensor_tensor(
                    out=slope[:, cubic], in0=b_of, in1=per_tile(square_term[:, cubic, :]), op=ALU.add
                )
                nc.vector.tensor_tensor(
                    out=offset[:, cubic], in0=b_of, in1=per_tile(linear[:, cubic, :]), op=ALU.mult
                )
            nc.vector.tensor_tensor(
                out=offset[:, NUM], in0=offset[:, NUM], in1=per_tile(constant[:]), op=ALU.add
            )
            absolute_value(magnitude, leading)

        def run(stage, step, at, count):
            if 0 <= step - at < count:
                stage(step - at)

        def quantise_if_complete(j):
            if j % ROW_TILES == ROW_TILES - 1:
                quantise_x(j // ROW_TILES)

        for step in range(AT_TURN_X, TILES + AT_FINISH):
            run(load_x, step, AT_LOAD, PIECES)
            run(absolute, step, AT_ABS, TILES)
            run(lambda t: square(t, nc.scalar), step, AT_SQUARE, TILES)
            run(square_y, step, AT_SQUARE_Y, TILES)
            run(root, step, AT_ROOT, TILES)
            run(lambda j: group_x(j, False), step, AT_GROUP_X, PIECES)
            run(lambda t: affine(t, DEN), step, AT_AFFINE, TILES)
            run(lambda t: square(t, nc.gpsimd), step, AT_ROOT, TILES)
            run(lambda t: affine(t, NUM), step, AT_AFFINE, TILES)
            run(lambda t: product(t, DEN), step, AT_PRODUCT, TILES)
            run(lambda t: product(t, NUM), step, AT_PRODUCT, TILES)
            run(quantise_if_complete, step, AT_QUANTISE, PIECES)
            if step == AT_QUANTISE + ROW_TILES - 1:
                make_tables()
            run(lambda j: group_x(j, True), step, AT_GROUP_X, PIECES)
            run(lambda t: square(t, nc.vector), step, AT_SQUARE, TILES)
            run(finish, step, AT_FINISH, TILES)
            run(turn_den, step, AT_TURN_DEN, TILES)
            run(lambda t: turn_num(t, range(ROW_TILES)), step, AT_TURN_NUM, TILES)
            run(multiply, step, AT_MULTIPLY, TILES)
            run(turn_x, step, AT_TURN_X, PIECES)
